import numpy as np
import ml_dtypes


def mxq(x, axis, fmt="e4m3"):
    dtype, down = {"e4m3": (ml_dtypes.float8_e4m3fn, 7), "e5m2": (ml_dtypes.float8_e5m2, 14)}[fmt]
    v = np.moveaxis(np.asarray(x, np.float32).astype(ml_dtypes.bfloat16).astype(np.float64), axis, -1)
    blocks = v.reshape(v.shape[:-1] + (-1, 32))
    amax = np.abs(blocks).max(-1, keepdims=True)
    byte = np.maximum(np.where(amax > 0, np.frexp(amax)[1] - 1 + 127, 0) - down, 1)
    scale = np.exp2(byte - 127.0)
    codes = (blocks / scale).astype(np.float32).astype(dtype).astype(np.float64)
    return np.moveaxis((codes * scale).reshape(v.shape), -1, axis)


WIDE = False


def mx_kscale(k):
    if not WIDE:
        return np.ones(k)
    levels = np.array([18, -18])
    if k % 512:
        return np.exp2(np.random.permutation(np.resize(levels, k // 32))).repeat(32)
    a = np.empty((k // 512, 16))
    for p in range(k // 512):
        a[p, :8] = np.random.permutation(np.resize(levels, 8))
        for g in range(8):
            far = levels[np.abs(levels - a[p, g]) >= 10]
            a[p, g + 8] = far[np.random.randint(len(far))]
    return np.exp2(a.ravel()).repeat(32)


BF16 = ml_dtypes.bfloat16


def bf(x):
    return np.asarray(x, np.float32).astype(BF16)


def f64(x):
    return np.asarray(x).astype(np.float64)


N, S, K, Yd, Xd = 1024, 4, 16, 1024, 512
LOG_2PI = np.log(2.0 * np.pi)


def sigmoid(v):
    return 1.0 / (1.0 + np.exp(-v))


def softplus(v):
    return np.maximum(v, 0.0) + np.log1p(np.exp(-np.abs(v)))


def log_softmax(v, axis):
    m = v - v.max(axis, keepdims=True)
    return m - np.log(np.exp(m).sum(axis, keepdims=True))


def mv_gaussian_log_prob(value, mu, sig_diags, event_shape):
    diff = value - mu
    M = np.sum((diff / sig_diags) ** 2, axis=-1)
    half_log_det = np.sum(np.log(sig_diags), axis=-1)
    return -0.5 * (event_shape * LOG_2PI + M) - half_log_det


def setup_inputs():
    s = mx_kscale(N)[:, None]
    u_mu = mx_kscale(Xd)
    u_sig = mx_kscale(Xd)
    c = min(np.min(u_mu), np.min(u_sig))
    Y0 = bf(np.random.standard_normal((N, Yd)) * 0.5)
    Wm0 = bf(np.random.standard_normal((Yd, Xd)) * 2.0 / np.sqrt(Yd))
    be_mu = bf(np.random.standard_normal(Xd) * 0.1)
    Ws0 = bf(np.random.standard_normal((Yd, Xd)) * 1.0 / np.sqrt(Yd))
    be_sig = bf(-3.0 + np.random.standard_normal(Xd) * 0.1)
    phi_mus = bf(np.random.standard_normal((K, Xd)) * 3.0 / np.sqrt(Xd))
    phi_sigs = bf(1.0 + (np.random.random_sample((K, Xd)) - 0.5) * 9.0 / np.sqrt(Xd))
    phi_logits = bf(np.random.standard_normal(K))
    g0 = bf(np.random.standard_normal((N, Xd)) * np.exp2(np.random.randint(-6, 1, (N, 1))) * 0.5 / s * u_mu)
    g1 = bf(np.random.standard_normal((N, Xd)) * np.exp2(np.random.randint(-6, 1, (N, 1))) * 16.0 / s * u_sig)
    g2 = bf(np.random.standard_normal((N, K)) * np.exp2(np.random.randint(-6, 1, (N, 1))) * 0.5 / s * c)
    enc_mu = f64(Y0) @ f64(Wm0) + f64(be_mu)
    sig_pre = f64(Y0) @ f64(Ws0) + f64(be_sig)
    std_k = (softplus(sig_pre) + 1e-3)[:, None, :] + f64(phi_sigs)[None, :, :]
    z_logits = log_softmax(f64(phi_logits), -1)[None, :] + mv_gaussian_log_prob(
        enc_mu[:, None, :], f64(phi_mus)[None, :, :], std_k, Xd)
    z_log_probs = log_softmax(z_logits, -1)
    return {"Y": bf(f64(Y0) * s),
            "We_mu": bf(f64(Wm0) / u_mu),
            "be_mu": be_mu,
            "We_sig": bf(f64(Ws0) / u_sig),
            "be_sig": be_sig,
            "phi_mus": phi_mus,
            "phi_sigs": phi_sigs,
            "phi_logits": phi_logits,
            "enc_mu": np.asarray(enc_mu, np.float32),
            "sig_pre": np.asarray(sig_pre, np.float32),
            "z_log_probs": np.asarray(z_log_probs, np.float32),
            "grad_0": g0, "grad_1": g1, "grad_2": g2}


def reference(Y, We_mu, be_mu, We_sig, be_sig, phi_mus, phi_sigs, phi_logits,
              enc_mu, sig_pre, z_log_probs, grad_0, grad_1, grad_2):
    mu = f64(enc_mu)
    a = f64(sig_pre)
    enc_sig = softplus(a) + 1e-3
    pm, ps = f64(phi_mus), f64(phi_sigs)
    g2 = f64(grad_2)
    dl = g2 - np.exp(f64(z_log_probs)) * g2.sum(-1, keepdims=True)
    dz_mu = f64(grad_0)
    d_sig = f64(grad_1)
    for k in range(K):
        std = enc_sig + ps[k][None, :]
        r = (mu - pm[k][None, :]) / std
        dk = dl[:, k:k + 1]
        dz_mu = dz_mu - dk * r / std
        d_sig = d_sig + dk * (r * r - 1.0) / std
    dz_sig = d_sig * sigmoid(a)
    dz = np.concatenate([dz_mu, dz_sig], axis=1)
    w = np.concatenate([f64(We_mu), f64(We_sig)], axis=1)
    dY = mxq(dz, 1, "e5m2") @ mxq(w, 1, "e4m3").T
    Yq = mxq(f64(Y), 0, "e4m3")
    dW_mu = Yq.T @ mxq(dz_mu, 0, "e5m2")
    dW_sig = Yq.T @ mxq(dz_sig, 0, "e5m2")
    return dY, dW_mu, dW_sig

@@ -1,0 +1,464 @@
+from contextlib import ExitStack
+
+import concourse.mybir as mybir
+from concourse.masks import make_identity
+
+N, KC, YD, XD = 1024, 16, 1024, 512
+FLOPS = 2 * 2 * N * YD * 2 * XD
+
+F32 = mybir.dt.float32
+BF16 = mybir.dt.bfloat16
+U32 = mybir.dt.uint32
+U8 = mybir.dt.uint8
+E4M3 = mybir.dt.float8_e4m3fn_x4
+E5M2 = mybir.dt.float8_e5m2_x4
+ALU = mybir.AluOpType
+ACT = mybir.ActivationFunctionType
+
+P = 128
+PACK = 4
+GROUP = P * PACK
+HALF = XD // 2
+CHUNKS = 4
+STEPS = CHUNKS * KC
+AHEAD = 2
+P_FLOOR = 2.0 ** -60
+BANKS = ("mu0", "mu1", "sum_mu0", "sum_mu1", "sum_sig0", "sum_sig1", "spare", "dl")
+
+
+def tile_deepgmm_pa_v_kernel(tc, Y, We_mu, be_mu, We_sig, be_sig, phi_mus, phi_sigs, phi_logits,
+                                          enc_mu, sig_pre, z_log_probs, grad_0, grad_1, grad_2,
+                                          out_0, out_1, out_2):
+    nc = tc.nc
+
+    def chunk_rows(dram, c):
+        g, fh = divmod(c, 2)
+        return dram.rearrange("(g p t) w -> g p t w", g=2, t=PACK)[g, :, :, fh * HALF:(fh + 1) * HALF]
+
+    def cols(n, width=P):
+        return slice(n * width, (n + 1) * width)
+
+    with ExitStack() as ctx:
+        keep = ctx.enter_context(tc.tile_pool(name="keep", bufs=1))
+        work = ctx.enter_context(tc.tile_pool(name="work", bufs=1))
+        psum = ctx.enter_context(tc.psum_pool(name="psum", bufs=1))
+        ctx.enter_context(tc.manual_schedule())
+
+        def bank(tag, dtype=F32):
+            return psum.tile([P, GROUP], dtype, name=tag, tag=tag)
+
+        def big(shape, dtype, name):
+            return work.tile(shape, dtype, name=name, tag="big", bufs=4, align_bytes=64)
+
+        def mid(shape, dtype, name):
+            return work.tile(shape, dtype, name=name, tag="mid", bufs=3, align_bytes=64)
+
+        def to_quantize(name):
+            return work.tile([P, PACK * YD], BF16, name=name, tag="to_quantize", bufs=1, align_bytes=64)
+
+        def mx_pair(name, width, bufs):
+            codes = work.tile([P, width], U32, name=name + "_codes", tag=name + "_codes", bufs=bufs, align_bytes=64)
+            scales = work.tile([P, width], U8, name=name + "_scales", tag=name + "_scales", bufs=bufs, align_bytes=64)
+            return codes, scales
+
+        a_raw = [keep.tile([P, PACK, HALF], F32, name="a_raw%d" % c) for c in range(CHUNKS)]
+        phi = keep.tile([P, XD], BF16, name="phi")
+        zlp = keep.tile([P, 2, PACK * KC], F32, name="zlp")
+        g2 = keep.tile([P, 2, PACK * KC], BF16, name="g2")
+        mu_raw, g0_raw, g1_raw, y_raw, w_raw = {}, {}, {}, {}, {}
+
+        def load_chunk(c):
+            mu_raw[c] = work.tile([P, PACK, HALF], F32, name="mu_raw", tag="mu_raw", bufs=1)
+            g0_raw[c] = work.tile([P, PACK, HALF], BF16, name="g0_raw", tag="g0_raw", bufs=1)
+            g1_raw[c] = work.tile([P, PACK, HALF], BF16, name="g1_raw", tag="g1_raw", bufs=1)
+            nc.sync.dma_start(out=mu_raw[c][:], in_=chunk_rows(enc_mu, c))
+            nc.sync.dma_start(out=g1_raw[c][:], in_=chunk_rows(grad_1, c))
+            nc.sync.dma_start(out=g0_raw[c][:], in_=chunk_rows(grad_0, c))
+
+        def load_y(g):
+            y_raw[g] = big([P, PACK, YD], BF16, "y_raw")
+            nc.sync.dma_start(out=y_raw[g][:], in_=Y.rearrange("(g p t) w -> g p t w", g=2, t=PACK)[g])
+
+        def load_w(fh):
+            w_raw[fh] = big([P, YD // P, 2 * HALF], BF16, "w_raw")
+            for part, weight in enumerate((We_mu, We_sig)):
+                nc.sync.dma_start(out=w_raw[fh][:, :, cols(part, HALF)],
+                                  in_=weight.rearrange("(y p) c -> p y c", p=P)[:, :, cols(fh, HALF)])
+
+        nc.vector.memset(phi[:], 0.0)
+        nc.sync.dma_start(out=a_raw[0][:], in_=chunk_rows(sig_pre, 0))
+        nc.sync.dma_start(out=phi[0:KC, :], in_=phi_sigs)
+        nc.sync.dma_start(out=phi[KC:2 * KC, :], in_=phi_mus)
+        nc.sync.dma_start(out=zlp[:], in_=z_log_probs.rearrange("(g p t) k -> p g (t k)", g=2, t=PACK))
+        nc.sync.dma_start(out=g2[:], in_=grad_2.rearrange("(g p t) k -> p g (t k)", g=2, t=PACK))
+        load_chunk(0)
+        load_y(0)
+        for c in range(1, CHUNKS):
+            nc.sync.dma_start(out=a_raw[c][:], in_=chunk_rows(sig_pre, c))
+        load_y(1)
+        load_w(0)
+        load_w(1)
+
+        ident = keep.tile([P, P], F32, name="ident")
+        ident_bf = keep.tile([P, P], BF16, name="ident_bf")
+        minus_ident_bf = keep.tile([P, P], BF16, name="minus_ident_bf")
+        make_identity(nc, ident_bf[:])
+        make_identity(nc, ident[:])
+        nc.vector.tensor_scalar(out=minus_ident_bf[:], in0=ident_bf[:], scalar1=-1.0, scalar2=None, op0=ALU.mult)
+
+        soft, ln_s = {}, {}
+
+        def flat(tile3):
+            return tile3[:].rearrange("p a b -> p (a b)")
+
+        def soft_abs(c):
+            soft[c] = mid([P, PACK, HALF], F32, "soft")
+            nc.scalar.activation(out=flat(soft[c]), in_=flat(a_raw[c]), func=ACT.Abs)
+
+        def soft_exp(c):
+            nc.scalar.activation(out=flat(soft[c]), in_=flat(soft[c]), func=ACT.Exp, scale=-1.0)
+
+        def soft_log1p(c):
+            nc.scalar.activation(out=flat(soft[c]), in_=flat(soft[c]), func=ACT.Ln, bias=1.0)
+
+        def soft_add_relu(c):
+            nc.vector.scalar_tensor_tensor(out=flat(soft[c]), in0=flat(a_raw[c]), scalar=0.0, in1=flat(soft[c]),
+                                           op0=ALU.max, op1=ALU.add)
+
+        def soft_log(c):
+            nc.scalar.activation(out=flat(soft[c]), in_=flat(soft[c]), func=ACT.Ln, bias=1e-3)
+
+        def features_first(src, j, tag):
+            dst = bank(tag)
+            for t in range(PACK):
+                nc.tensor.transpose(dst[:, cols(t)], src[:, t, cols(j)], ident[:])
+            return dst
+
+        def new_ln_s(c):
+            ln_s[c] = keep.tile([P, 2, GROUP], F32, name="ln_s%d" % c)
+
+        phi_ps = bank("spare", BF16)
+        for J in range(XD // P):
+            nc.tensor.transpose(phi_ps[:, cols(J)], phi[:, cols(J)], ident_bf[:])
+        phi_t = keep.tile([P, XD // P, 2 * KC], F32, name="phi_t")
+        nc.vector.tensor_copy(out=phi_t[:], in_=phi_ps[:].rearrange("d (J r) -> d J r", r=P)[:, :, 0:2 * KC])
+
+        def small(name):
+            return keep.tile([P, XD // P, KC], F32, name=name)
+
+        p_c, ln_p, inv_p, minus_inv_p2 = small("p_c"), small("ln_p"), small("inv_p"), small("minus_inv_p2")
+        sig_lo, sig_hi, guess, polish, rsqrt_p = small("sig_lo"), small("sig_hi"), small("guess"), small("polish"), small("rsqrt_p")
+        nc.vector.tensor_scalar(out=p_c[:], in0=phi_t[:, :, 0:KC], scalar1=P_FLOOR, scalar2=None, op0=ALU.max)
+        nc.vector.reciprocal(out=inv_p[:], in_=p_c[:])
+
+        prob = keep.tile([P, 2 * PACK, KC], F32, name="prob")
+        g2_sum = keep.tile([P, 2 * PACK], F32, name="g2_sum")
+        dl = keep.tile([P, 2 * PACK, KC], F32, name="dl")
+        g2_rows = g2[:].rearrange("p g (t k) -> p (g t) k", k=KC)
+        soft_abs(0)
+        nc.scalar.activation(out=flat(prob), in_=flat(zlp), func=ACT.Exp)
+        soft_exp(0)
+        nc.vector.tensor_reduce(out=g2_sum[:], in_=g2_rows, axis=mybir.AxisListType.X, op=ALU.add)
+        nc.vector.scalar_tensor_tensor(out=flat(minus_inv_p2), in0=flat(inv_p), scalar=-1.0, in1=flat(inv_p),
+                                       op0=ALU.mult, op1=ALU.mult)
+        nc.vector.tensor_tensor(out=prob[:], in0=prob[:], in1=g2_sum[:].unsqueeze(2).to_broadcast([P, 2 * PACK, KC]),
+                                op=ALU.mult)
+        nc.vector.tensor_tensor(out=dl[:], in0=g2_rows, in1=prob[:], op=ALU.subtract)
+
+        soft_log1p(0)
+        nc.scalar.activation(out=flat(ln_p), in_=flat(p_c), func=ACT.Ln)
+        soft_add_relu(0)
+
+        mu_ps, dl_ps, sum_mu, sum_sig = {}, {}, {}, {}
+
+        def mu_features_first(c):
+            for j in range(2):
+                mu_ps[c, j] = features_first(mu_raw[c], j, "mu%d" % j)
+
+        def spread_dl(i):
+            c, k = divmod(i, KC)
+            dl_ps[i] = bank("dl")
+            for t in range(PACK):
+                column = dl[:, PACK * (c // 2) + t, k:k + 1]
+                nc.tensor.transpose(dl_ps[i][:, cols(t)], column.to_broadcast([P, P]), ident[:])
+
+        def open_sums(sums, tag, c, sign, grad):
+            for j in range(2):
+                sums[c, j] = bank("%s%d" % (tag, j))
+                nc.tensor.matmul(sums[c, j][:].rearrange("p (t d) -> p t d", t=PACK), lhsT=sign[:],
+                                 rhs=grad[c][:, :, cols(j)], start=True, stop=False)
+
+        mu_features_first(0)
+        spread_dl(0)
+        new_ln_s(0)
+        for j in range(2):
+            head_ps = features_first(soft[0], j, "sum_mu%d" % j)
+            nc.scalar.activation(out=ln_s[0][:, j, :], in_=head_ps[:], func=ACT.Ln, bias=1e-3)
+        open_sums(sum_sig, "sum_sig", 0, minus_ident_bf, g1_raw)
+        open_sums(sum_mu, "sum_mu", 0, ident_bf, g0_raw)
+
+        nc.scalar.activation(out=flat(sig_lo), in_=flat(ln_p), func=ACT.Sigmoid, scale=-0.5)
+        nc.scalar.activation(out=flat(sig_hi), in_=flat(ln_p), func=ACT.Sigmoid, scale=0.5)
+
+        y_mx, w_mx, dz_tok_mx, dz_feat_mx = {}, {}, {}, {}
+
+        def quantize(pair, src, fmt):
+            nc.vector.quantize_mx(out=pair[0][:].bitcast(fmt), scales=pair[1][:], in_=src)
+
+        def quantize_y(g):
+            grouped = to_quantize("y_grouped")
+            nc.vector.tensor_copy(out=grouped[:].rearrange("p (c i t) -> p c t i", i=4, t=PACK),
+                                  in_=y_raw[g][:].rearrange("p t (c i) -> p c t i", i=4))
+            y_mx[g] = mx_pair("y", YD, 2)
+            return lambda: quantize(y_mx[g], grouped[:], E4M3)
+
+        finish_y0 = quantize_y(0)
+        nc.vector.reciprocal(out=sig_hi[:], in_=sig_hi[:])
+        finish_y0()
+        nc.vector.tensor_tensor(out=guess[:], in0=sig_lo[:], in1=sig_hi[:], op=ALU.mult)
+        nc.vector.scalar_tensor_tensor(out=flat(polish), in0=flat(guess), scalar=-0.5, in1=flat(guess),
+                                       op0=ALU.mult, op1=ALU.mult)
+        nc.vector.tensor_tensor(out=polish[:], in0=polish[:], in1=p_c[:], op=ALU.mult)
+        nc.vector.scalar_tensor_tensor(out=flat(rsqrt_p), in0=flat(polish), scalar=1.5, in1=flat(guess),
+                                       op0=ALU.add, op1=ALU.mult)
+
+        share, weight, resid, square = {}, {}, {}, {}
+
+        def pair_tile(name, bufs):
+            return work.tile([P, 2, GROUP], F32, name=name, tag=name, bufs=bufs)
+
+        def per_feature(table, i, j):
+            c, k = divmod(i, KC)
+            return table[:, 2 * (c % 2) + j, k:k + 1]
+
+        def stage_share(i):
+            share[i] = pair_tile("share", 4)
+            for j in range(2):
+                nc.scalar.activation(out=share[i][:, j, :], in_=ln_s[i // KC][:, j, :], func=ACT.Sigmoid,
+                                     scale=-1.0, bias=per_feature(ln_p, i, j))
+
+        def stage_front(i):
+            weight[i] = pair_tile("weight", 5)
+            resid[i] = pair_tile("resid", 4)
+            for j in range(2):
+                nc.vector.scalar_tensor_tensor(out=weight[i][:, j, :], in0=share[i][:, j, :],
+                                               scalar=per_feature(minus_inv_p2, i, j), in1=dl_ps[i][:],
+                                               op0=ALU.mult, op1=ALU.mult)
+            for j in range(2):
+                nc.vector.scalar_tensor_tensor(out=resid[i][:, j, :], in0=mu_ps[i // KC, j][:],
+                                               scalar=per_feature(phi_t[:, :, KC:2 * KC], i, j), in1=share[i][:, j, :],
+                                               op0=ALU.subtract, op1=ALU.mult)
+
+        def stage_square(i):
+            square[i] = pair_tile("square", 4)
+            for j in range(2):
+                nc.scalar.activation(out=square[i][:, j, :], in_=resid[i][:, j, :], func=ACT.Square,
+                                     scale=per_feature(rsqrt_p, i, j))
+
+        def stage_back(i):
+            for j in range(2):
+                nc.vector.scalar_tensor_tensor(out=square[i][:, j, :], in0=square[i][:, j, :],
+                                               scalar=per_feature(p_c, i, j), in1=weight[i][:, j, :],
+                                               op0=ALU.subtract, op1=ALU.mult)
+            nc.gpsimd.tensor_tensor(out=flat(weight[i]), in0=flat(weight[i]), in1=flat(resid[i]), op=ALU.mult)
+
+        def stage_add(sums, terms, i):
+            c, k = divmod(i, KC)
+            for j in range(2):
+                for t in range(PACK):
+                    nc.tensor.matmul(sums[c, j][:, cols(t)], lhsT=terms[i][:, j, cols(t)], rhs=ident[:],
+                                     is_transpose=True, start=False, stop=(k == KC - 1 and t == PACK - 1))
+
+        gate, dz_tok, dz_feat, w_grouped, staged = {}, {}, {}, {}, {}
+
+        def ln_s_half(c, j):
+            if j == 0:
+                new_ln_s(c)
+            turned = features_first(soft[c], j, "spare")
+            return lambda: nc.scalar.copy(out=ln_s[c][:, j, :], in_=turned[:])
+
+        def gate_half(c, j):
+            if j == 0:
+                gate[c] = work.tile([P, HALF, PACK], F32, name="gate", tag="gate", bufs=1)
+            nc.scalar.activation(out=gate[c][:, cols(j), :], in_=a_raw[c][:, :, cols(j)].rearrange("p t d -> p d t"),
+                                 func=ACT.Sigmoid)
+
+        def round_dz_sig(c):
+            dz_tok[c] = mid([P, 2 * HALF, PACK], BF16, "dz_tok")
+            for j in range(2):
+                nc.vector.scalar_tensor_tensor(out=dz_tok[c][:, cols(2 + j), :],
+                                               in0=sum_sig[c, j][:].rearrange("p (t d) -> p d t", t=PACK),
+                                               scalar=-1.0, in1=gate[c][:, cols(j), :], op0=ALU.mult, op1=ALU.mult)
+
+        def round_dz_mu(c):
+            for j in range(2):
+                nc.scalar.copy(out=dz_tok[c][:, cols(j), :],
+                               in_=sum_mu[c, j][:].rearrange("p (t d) -> p d t", t=PACK))
+
+        def quantize_dz_tok(c):
+            dz_tok_mx[c] = mx_pair("dz_tok", GROUP, CHUNKS)
+            quantize(dz_tok_mx[c], flat(dz_tok[c]), E5M2)
+
+        def dz_feat_half(c, u, tag, copy):
+            if u == 0:
+                dz_feat[c] = mid([P, GROUP, PACK], BF16, "dz_feat")
+            words = flat(dz_tok[c]).bitcast(F32)
+            turned = bank(tag)
+            for f in range(PACK):
+                nc.tensor.transpose(turned[:, cols(f)], words[:, 2 * f + u:2 * GROUP:2 * PACK], ident[:])
+            return lambda: copy(out=dz_feat[c][:, cols(u, 2 * P), :].rearrange("q (e p) f -> q e p f", e=2),
+                                in_=turned[:].bitcast(BF16).rearrange("q (f p e) -> q e p f", f=PACK, e=2))
+
+        def quantize_dz_feat(c):
+            dz_feat_mx[c] = mx_pair("dz_feat", GROUP, 2)
+            quantize(dz_feat_mx[c], flat(dz_feat[c]), E5M2)
+
+        def w_quarter(fh, n):
+            if n == 0:
+                w_grouped[fh] = to_quantize("w_grouped")
+            words = flat(w_raw[fh]).bitcast(F32)
+            turned = bank("spare")
+            for y in range(2):
+                for u in range(2):
+                    first = HALF * (2 * n + y)
+                    nc.tensor.transpose(turned[:, cols(2 * y + u)], words[:, first + u:first + HALF:2], ident[:])
+            return lambda: nc.scalar.copy(
+                out=w_grouped[fh][:].bitcast(F32)[:, cols(n, GROUP)].rearrange("q (y p u) -> q y p u", y=2, u=2),
+                in_=turned[:].rearrange("q (y u p) -> q y p u", y=2, u=2))
+
+        def quantize_w(fh):
+            w_mx[fh] = mx_pair("w", YD, 2)
+            quantize(w_mx[fh], w_grouped[fh][:], E4M3)
+
+        def mx_group(tag, passes):
+            acc = bank(tag)
+            for n, (lhs, lhs_cols, lhs_fmt, rhs, rhs_cols, rhs_fmt) in enumerate(passes):
+                nc.tensor.matmul_mx(out=acc[:], lhsT=lhs[0][:, lhs_cols].bitcast(lhs_fmt), lhsT_scale=lhs[1][:, lhs_cols],
+                                    rhs=rhs[0][:, rhs_cols].bitcast(rhs_fmt), rhs_scale=rhs[1][:, rhs_cols],
+                                    start=(n == 0), stop=(n == len(passes) - 1))
+            return acc
+
+        def dy_group(g, n, tag, copy):
+            t, h = divmod(n, 2)
+            acc = mx_group(tag, [(dz_feat_mx[2 * g + fh], cols(t), E5M2, w_mx[fh], cols(h, GROUP), E4M3)
+                                 for fh in range(2)])
+
+            def finish():
+                if h == 0:
+                    staged["dy", g, t] = big([P, 2, GROUP], F32, "dy_staged")
+                copy(out=staged["dy", g, t][:, h, :], in_=acc[:])
+                if h == 1:
+                    nc.sync.dma_start(out=out_0.rearrange("(g p t) y -> g t p y", g=2, t=PACK)[g, t],
+                                      in_=flat(staged["dy", g, t]))
+            return finish
+
+        def dw_group(fh, n, tag, copy):
+            pair, h = divmod(n, 2)
+            acc = mx_group(tag, [(y_mx[g], cols(n), E4M3, dz_tok_mx[2 * g + fh], cols(0, GROUP), E5M2)
+                                 for g in range(2)])
+
+            def finish():
+                if h == 0:
+                    staged["dw", fh, pair] = big([P, 2, GROUP], F32, "dw_staged")
+                copy(out=staged["dw", fh, pair][:, h, :], in_=acc[:])
+                if h == 1:
+                    for part, dst in enumerate((out_1, out_2)):
+                        rows = dst.rearrange("(y p) d -> p y d", p=P)
+                        nc.sync.dma_start(out=rows[:, 2 * pair:2 * pair + 2, cols(fh, HALF)],
+                                          in_=staged["dw", fh, pair][:, :, cols(part, HALF)])
+            return finish
+
+        EXP_STEP, LOG_STEP = 2, 6
+        spare_jobs = {}
+        for n in range(2 * (CHUNKS - 1)):
+            spare_jobs[LOG_STEP + 2 + n] = lambda n=n: ln_s_half(1 + n // 2, n % 2)
+        for c in range(CHUNKS - 1):
+            for u in range(2):
+                spare_jobs[KC * (c + 1) + 2 + u] = lambda c=c, u=u: dz_feat_half(c, u, "spare", nc.scalar.copy)
+        for n in range(8):
+            spare_jobs[KC + 4 + n] = lambda n=n: w_quarter(n // 4, n % 4)
+            spare_jobs[2 * KC + 5 + n] = lambda n=n: dy_group(0, n, "spare", nc.scalar.copy)
+            spare_jobs[3 * KC + 4 + n] = lambda n=n: dw_group(0, n, "spare", nc.scalar.copy)
+
+        def live(i):
+            return 0 <= i < STEPS
+
+        waiting_copy = []
+        put_off = []
+        for s in range(-2 * AHEAD, STEPS + 2):
+            closing = (s - 2) // KC if live(s - 2) and (s - 2) % KC == KC - 1 else None
+            scalar_away = LOG_STEP < s <= LOG_STEP + 1
+            if not scalar_away:
+                for job in put_off:
+                    job()
+                put_off.clear()
+            if live(s + 2 * AHEAD):
+                if scalar_away:
+                    put_off.append(lambda i=s + 2 * AHEAD: stage_share(i))
+                else:
+                    stage_share(s + 2 * AHEAD)
+            for job in waiting_copy:
+                job()
+            waiting_copy.clear()
+            if 0 <= s < CHUNKS - 1:
+                soft_abs(s + 1)
+            if live(s) and s % KC >= KC - 2:
+                gate_half(s // KC, s % 2)
+            if live(s - 2):
+                if (s - 2) % KC == 0 and s > 2:
+                    open_sums(sum_mu, "sum_mu", (s - 2) // KC, ident_bf, g0_raw)
+                stage_add(sum_mu, weight, s - 2)
+            if closing is not None:
+                round_dz_sig(closing)
+                round_dz_mu(closing)
+            if live(s + AHEAD):
+                stage_front(s + AHEAD)
+            if live(s + AHEAD + 1) and s + AHEAD + 1 > 0:
+                spread_dl(s + AHEAD + 1)
+            if live(s + AHEAD):
+                if scalar_away:
+                    put_off.append(lambda i=s + AHEAD: stage_square(i))
+                else:
+                    stage_square(s + AHEAD)
+            if live(s - 1):
+                if (s - 1) % KC == 0 and s > 1:
+                    open_sums(sum_sig, "sum_sig", (s - 1) // KC, minus_ident_bf, g1_raw)
+                stage_add(sum_sig, square, s - 1)
+            if live(s + AHEAD + 1) and (s + AHEAD + 1) % KC == 0 and s > 0:
+                mu_features_first((s + AHEAD + 1) // KC)
+            if s == EXP_STEP:
+                for c in range(1, CHUNKS):
+                    soft_exp(c)
+            if s == LOG_STEP:
+                for c in range(1, CHUNKS):
+                    soft_log1p(c)
+            if s == LOG_STEP + 1:
+                finish_y1 = quantize_y(1)
+                for c in range(1, CHUNKS):
+                    soft_add_relu(c)
+                    soft_log(c)
+                finish_y1()
+            if live(s) and s >= KC and s % KC == 2:
+                quantize_dz_tok(s // KC - 1)
+            if live(s) and s >= KC and s % KC == 4:
+                quantize_dz_feat(s // KC - 1)
+            if s in (KC + 8, KC + 12):
+                quantize_w((s - KC - 8) // 4)
+            if live(s):
+                stage_back(s)
+            if s in spare_jobs:
+                waiting_copy.append(spare_jobs[s]())
+            if live(s) and s % KC == 4 and s // KC + 1 < CHUNKS:
+                load_chunk(s // KC + 1)
+
+        last = CHUNKS - 1
+        copy_lo = dz_feat_half(last, 0, "spare", nc.scalar.copy)
+        copy_hi = dz_feat_half(last, 1, "dl", nc.vector.tensor_copy)
+        quantize_dz_tok(last)
+        copy_lo()
+        copy_hi()
+        quantize_dz_feat(last)
+        for n in range(16):
+            copy = nc.scalar.copy if n % 2 == 0 else nc.vector.tensor_copy
+            group = dw_group if n < 8 else dy_group
+            group(1, n % 8, BANKS[n % 8], copy)()

@@ -48,7 +48,7 @@ def tile_deepgmm_pa_v_kernel(tc, Y, We_mu, be_mu, We_sig, be_sig, phi_mus, phi_s
             return psum.tile([P, GROUP], dtype, name=tag, tag=tag)
 
         def big(shape, dtype, name):
-            return work.tile(shape, dtype, name=name, tag="big", bufs=4, align_bytes=64)
+            return work.tile(shape, dtype, name=name, tag="big", bufs=5, align_bytes=64)
 
         def mid(shape, dtype, name):
             return work.tile(shape, dtype, name=name, tag="mid", bufs=3, align_bytes=64)
@@ -86,7 +86,8 @@ def tile_deepgmm_pa_v_kernel(tc, Y, We_mu, be_mu, We_sig, be_sig, phi_mus, phi_s
                                   in_=weight.rearrange("(y p) c -> p y c", p=P)[:, :, cols(fh, HALF)])
 
         nc.vector.memset(phi[:], 0.0)
-        nc.sync.dma_start(out=a_raw[0][:], in_=chunk_rows(sig_pre, 0))
+        for j in range(2):
+            nc.sync.dma_start(out=a_raw[0][:, :, cols(j)], in_=chunk_rows(sig_pre, 0)[:, :, cols(j)])
         nc.sync.dma_start(out=phi[0:KC, :], in_=phi_sigs)
         nc.sync.dma_start(out=phi[KC:2 * KC, :], in_=phi_mus)
         nc.sync.dma_start(out=zlp[:], in_=z_log_probs.rearrange("(g p t) k -> p g (t k)", g=2, t=PACK))
@@ -95,9 +96,9 @@ def tile_deepgmm_pa_v_kernel(tc, Y, We_mu, be_mu, We_sig, be_sig, phi_mus, phi_s
         load_y(0)
         for c in range(1, CHUNKS):
             nc.sync.dma_start(out=a_raw[c][:], in_=chunk_rows(sig_pre, c))
-        load_y(1)
         load_w(0)
         load_w(1)
+        load_y(1)
 
         ident = keep.tile([P, P], F32, name="ident")
         ident_bf = keep.tile([P, P], BF16, name="ident_bf")
@@ -137,6 +138,11 @@ def tile_deepgmm_pa_v_kernel(tc, Y, We_mu, be_mu, We_sig, be_sig, phi_mus, phi_s
         def new_ln_s(c):
             ln_s[c] = keep.tile([P, 2, GROUP], F32, name="ln_s%d" % c)
 
+        soft[0] = mid([P, PACK, HALF], F32, "soft")
+        for j in range(2):
+            nc.vector.scalar_tensor_tensor(out=soft[0][:, :, cols(j)], in0=a_raw[0][:, :, cols(j)], scalar=-1.0,
+                                           in1=a_raw[0][:, :, cols(j)], op0=ALU.mult, op1=ALU.min)
+            nc.scalar.activation(out=soft[0][:, :, cols(j)], in_=soft[0][:, :, cols(j)], func=ACT.Exp)
         phi_ps = bank("spare", BF16)
         for J in range(XD // P):
             nc.tensor.transpose(phi_ps[:, cols(J)], phi[:, cols(J)], ident_bf[:])
@@ -155,9 +161,7 @@ def tile_deepgmm_pa_v_kernel(tc, Y, We_mu, be_mu, We_sig, be_sig, phi_mus, phi_s
         g2_sum = keep.tile([P, 2 * PACK], F32, name="g2_sum")
         dl = keep.tile([P, 2 * PACK, KC], F32, name="dl")
         g2_rows = g2[:].rearrange("p g (t k) -> p (g t) k", k=KC)
-        soft_abs(0)
         nc.scalar.activation(out=flat(prob), in_=flat(zlp), func=ACT.Exp)
-        soft_exp(0)
         nc.vector.tensor_reduce(out=g2_sum[:], in_=g2_rows, axis=mybir.AxisListType.X, op=ALU.add)
         nc.vector.scalar_tensor_tensor(out=flat(minus_inv_p2), in0=flat(inv_p), scalar=-1.0, in1=flat(inv_p),
                                        op0=ALU.mult, op1=ALU.mult)
@@ -165,9 +169,11 @@ def tile_deepgmm_pa_v_kernel(tc, Y, We_mu, be_mu, We_sig, be_sig, phi_mus, phi_s
                                 op=ALU.mult)
         nc.vector.tensor_tensor(out=dl[:], in0=g2_rows, in1=prob[:], op=ALU.subtract)
 
-        soft_log1p(0)
+        for j in range(2):
+            nc.scalar.activation(out=soft[0][:, :, cols(j)], in_=soft[0][:, :, cols(j)], func=ACT.Ln, bias=1.0)
+            nc.vector.scalar_tensor_tensor(out=soft[0][:, :, cols(j)], in0=a_raw[0][:, :, cols(j)], scalar=0.0,
+                                           in1=soft[0][:, :, cols(j)], op0=ALU.max, op1=ALU.add)
         nc.scalar.activation(out=flat(ln_p), in_=flat(p_c), func=ACT.Ln)
-        soft_add_relu(0)
 
         mu_ps, dl_ps, sum_mu, sum_sig = {}, {}, {}, {}
 
@@ -205,22 +211,32 @@ def tile_deepgmm_pa_v_kernel(tc, Y, We_mu, be_mu, We_sig, be_sig, phi_mus, phi_s
         def quantize(pair, src, fmt):
             nc.vector.quantize_mx(out=pair[0][:].bitcast(fmt), scales=pair[1][:], in_=src)
 
-        def quantize_y(g):
-            grouped = to_quantize("y_grouped")
-            nc.vector.tensor_copy(out=grouped[:].rearrange("p (c i t) -> p c t i", i=4, t=PACK),
-                                  in_=y_raw[g][:].rearrange("p t (c i) -> p c t i", i=4))
-            y_mx[g] = mx_pair("y", YD, 2)
-            return lambda: quantize(y_mx[g], grouped[:], E4M3)
+        y_grouped = {}
 
-        finish_y0 = quantize_y(0)
+        def group_y(g, n, parts, copy):
+            if n == 0:
+                y_grouped[g] = to_quantize("y_grouped")
+            width = YD // parts
+            copy(out=y_grouped[g][:, cols(n, PACK * width)].rearrange("p (c i t) -> p c t i", i=4, t=PACK),
+                 in_=y_raw[g][:, :, cols(n, width)].rearrange("p t (c i) -> p c t i", i=4))
+
+        def quantize_y(g):
+            y_mx[g] = mx_pair("y", YD, 2)
+            quantize(y_mx[g], y_grouped[g][:], E4M3)
+
+        group_y(0, 0, 1, nc.vector.tensor_copy)
         nc.vector.reciprocal(out=sig_hi[:], in_=sig_hi[:])
-        finish_y0()
-        nc.vector.tensor_tensor(out=guess[:], in0=sig_lo[:], in1=sig_hi[:], op=ALU.mult)
-        nc.vector.scalar_tensor_tensor(out=flat(polish), in0=flat(guess), scalar=-0.5, in1=flat(guess),
-                                       op0=ALU.mult, op1=ALU.mult)
-        nc.vector.tensor_tensor(out=polish[:], in0=polish[:], in1=p_c[:], op=ALU.mult)
-        nc.vector.scalar_tensor_tensor(out=flat(rsqrt_p), in0=flat(polish), scalar=1.5, in1=flat(guess),
-                                       op0=ALU.add, op1=ALU.mult)
+        quantize_y(0)
+        warm_mx = mx_pair("warm", P, 1)
+        quantize(warm_mx, y_grouped[0][:, 0:GROUP], E5M2)
+        polish_steps = [
+            lambda: nc.vector.tensor_tensor(out=guess[:], in0=sig_lo[:], in1=sig_hi[:], op=ALU.mult),
+            lambda: nc.vector.scalar_tensor_tensor(out=flat(polish), in0=flat(guess), scalar=-0.5, in1=flat(guess),
+                                                   op0=ALU.mult, op1=ALU.mult),
+            lambda: nc.vector.tensor_tensor(out=polish[:], in0=polish[:], in1=p_c[:], op=ALU.mult),
+            lambda: nc.vector.scalar_tensor_tensor(out=flat(rsqrt_p), in0=flat(polish), scalar=1.5, in1=flat(guess),
+                                                   op0=ALU.add, op1=ALU.mult),
+        ]
 
         share, weight, resid, square = {}, {}, {}, {}
 
@@ -244,10 +260,14 @@ def tile_deepgmm_pa_v_kernel(tc, Y, We_mu, be_mu, We_sig, be_sig, phi_mus, phi_s
                 nc.vector.scalar_tensor_tensor(out=weight[i][:, j, :], in0=share[i][:, j, :],
                                                scalar=per_feature(minus_inv_p2, i, j), in1=dl_ps[i][:],
                                                op0=ALU.mult, op1=ALU.mult)
+                if i == 0:
+                    polish_steps[j]()
             for j in range(2):
                 nc.vector.scalar_tensor_tensor(out=resid[i][:, j, :], in0=mu_ps[i // KC, j][:],
                                                scalar=per_feature(phi_t[:, :, KC:2 * KC], i, j), in1=share[i][:, j, :],
                                                op0=ALU.subtract, op1=ALU.mult)
+                if i == 0:
+                    polish_steps[2 + j]()
 
         def stage_square(i):
             square[i] = pair_tile("square", 4)
@@ -260,7 +280,8 @@ def tile_deepgmm_pa_v_kernel(tc, Y, We_mu, be_mu, We_sig, be_sig, phi_mus, phi_s
                 nc.vector.scalar_tensor_tensor(out=square[i][:, j, :], in0=square[i][:, j, :],
                                                scalar=per_feature(p_c, i, j), in1=weight[i][:, j, :],
                                                op0=ALU.subtract, op1=ALU.mult)
-            nc.gpsimd.tensor_tensor(out=flat(weight[i]), in0=flat(weight[i]), in1=flat(resid[i]), op=ALU.mult)
+            engine = nc.gpsimd if i < STEPS - 1 else nc.vector
+            engine.tensor_tensor(out=flat(weight[i]), in0=flat(weight[i]), in1=flat(resid[i]), op=ALU.mult)
 
         def stage_add(sums, terms, i):
             c, k = divmod(i, KC)
@@ -383,11 +404,15 @@ def tile_deepgmm_pa_v_kernel(tc, Y, We_mu, be_mu, We_sig, be_sig, phi_mus, phi_s
         def live(i):
             return 0 <= i < STEPS
 
+        def keep_warm(tag):
+            mx_group(tag, [(warm_mx, cols(0), E5M2, y_mx[0], cols(0, GROUP), E4M3)])
+
+        Y_STEP = 2 * KC + 6
+        mx_job_steps = set(range(2 * KC + 5, 2 * KC + 13)) | set(range(3 * KC + 4, 3 * KC + 12))
         waiting_copy = []
         put_off = []
-        for s in range(-2 * AHEAD, STEPS + 2):
-            closing = (s - 2) // KC if live(s - 2) and (s - 2) % KC == KC - 1 else None
-            scalar_away = LOG_STEP < s <= LOG_STEP + 1
+        for s in range(-2 * AHEAD, STEPS + 1):
+            scalar_away = s == LOG_STEP + 1
             if not scalar_away:
                 for job in put_off:
                     job()
@@ -404,28 +429,30 @@ def tile_deepgmm_pa_v_kernel(tc, Y, We_mu, be_mu, We_sig, be_sig, phi_mus, phi_s
                 soft_abs(s + 1)
             if live(s) and s % KC >= KC - 2:
                 gate_half(s // KC, s % 2)
-            if live(s - 2):
-                if (s - 2) % KC == 0 and s > 2:
-                    open_sums(sum_mu, "sum_mu", (s - 2) // KC, ident_bf, g0_raw)
-                stage_add(sum_mu, weight, s - 2)
-            if closing is not None:
-                round_dz_sig(closing)
-                round_dz_mu(closing)
+            if Y_STEP <= s < Y_STEP + 8:
+                group_y(1, s - Y_STEP, 8, nc.scalar.copy)
+            if s > 1 and s % KC == 1:
+                round_dz_mu(s // KC - 1)
             if live(s + AHEAD):
                 stage_front(s + AHEAD)
+            if s > 0 and s % KC == 0:
+                round_dz_sig(s // KC - 1)
             if live(s + AHEAD + 1) and s + AHEAD + 1 > 0:
+                keep_warm("dl")
                 spread_dl(s + AHEAD + 1)
             if live(s + AHEAD):
                 if scalar_away:
                     put_off.append(lambda i=s + AHEAD: stage_square(i))
                 else:
                     stage_square(s + AHEAD)
-            if live(s - 1):
-                if (s - 1) % KC == 0 and s > 1:
-                    open_sums(sum_sig, "sum_sig", (s - 1) // KC, minus_ident_bf, g1_raw)
-                stage_add(sum_sig, square, s - 1)
             if live(s + AHEAD + 1) and (s + AHEAD + 1) % KC == 0 and s > 0:
                 mu_features_first((s + AHEAD + 1) // KC)
+            if live(s - 1):
+                if (s - 1) % KC == 0 and s > 1:
+                    open_sums(sum_mu, "sum_mu", (s - 1) // KC, ident_bf, g0_raw)
+                stage_add(sum_mu, weight, s - 1)
+            if live(s) and s not in mx_job_steps:
+                keep_warm("spare")
             if s == EXP_STEP:
                 for c in range(1, CHUNKS):
                     soft_exp(c)
@@ -433,25 +460,29 @@ def tile_deepgmm_pa_v_kernel(tc, Y, We_mu, be_mu, We_sig, be_sig, phi_mus, phi_s
                 for c in range(1, CHUNKS):
                     soft_log1p(c)
             if s == LOG_STEP + 1:
-                finish_y1 = quantize_y(1)
                 for c in range(1, CHUNKS):
                     soft_add_relu(c)
                     soft_log(c)
-                finish_y1()
             if live(s) and s >= KC and s % KC == 2:
                 quantize_dz_tok(s // KC - 1)
             if live(s) and s >= KC and s % KC == 4:
                 quantize_dz_feat(s // KC - 1)
             if s in (KC + 8, KC + 12):
                 quantize_w((s - KC - 8) // 4)
+            if s == Y_STEP + 8:
+                quantize_y(1)
             if live(s):
                 stage_back(s)
+                if s % KC == 0 and s > 0:
+                    open_sums(sum_sig, "sum_sig", s // KC, minus_ident_bf, g1_raw)
+                stage_add(sum_sig, square, s)
             if s in spare_jobs:
                 waiting_copy.append(spare_jobs[s]())
             if live(s) and s % KC == 4 and s // KC + 1 < CHUNKS:
                 load_chunk(s // KC + 1)
 
         last = CHUNKS - 1
+        round_dz_mu(last)
         copy_lo = dz_feat_half(last, 0, "spare", nc.scalar.copy)
         copy_hi = dz_feat_half(last, 1, "dl", nc.vector.tensor_copy)
         quantize_dz_tok(last)

@@ -21,7 +21,9 @@ GROUP = P * PACK
 HALF = XD // 2
 CHUNKS = 4
 STEPS = CHUNKS * KC
-AHEAD = 2
+AHEAD = 1
+LEAD = 5
+SPLIT = 448
 P_FLOOR = 2.0 ** -60
 BANKS = ("mu0", "mu1", "sum_mu0", "sum_mu1", "sum_sig0", "sum_sig1", "spare", "dl")
 
@@ -107,7 +109,7 @@ def tile_deepgmm_pa_v_kernel(tc, Y, We_mu, be_mu, We_sig, be_sig, phi_mus, phi_s
         make_identity(nc, ident[:])
         nc.vector.tensor_scalar(out=minus_ident_bf[:], in0=ident_bf[:], scalar1=-1.0, scalar2=None, op0=ALU.mult)
 
-        soft, ln_s = {}, {}
+        soft, ln_s, prepared = {}, {}, [0]
 
         def flat(tile3):
             return tile3[:].rearrange("p a b -> p (a b)")
@@ -116,15 +118,15 @@ def tile_deepgmm_pa_v_kernel(tc, Y, We_mu, be_mu, We_sig, be_sig, phi_mus, phi_s
             soft[c] = mid([P, PACK, HALF], F32, "soft")
             nc.scalar.activation(out=flat(soft[c]), in_=flat(a_raw[c]), func=ACT.Abs)
 
-        def soft_exp(c):
-            nc.scalar.activation(out=flat(soft[c]), in_=flat(soft[c]), func=ACT.Exp, scale=-1.0)
+        def soft_sigmoid(c):
+            nc.scalar.activation(out=flat(soft[c]), in_=flat(soft[c]), func=ACT.Sigmoid, scale=-1.0)
 
         def soft_log1p(c):
-            nc.scalar.activation(out=flat(soft[c]), in_=flat(soft[c]), func=ACT.Ln, bias=1.0)
+            nc.scalar.activation(out=flat(soft[c]), in_=flat(soft[c]), func=ACT.Ln, scale=-1.0, bias=1.0)
 
         def soft_add_relu(c):
             nc.vector.scalar_tensor_tensor(out=flat(soft[c]), in0=flat(a_raw[c]), scalar=0.0, in1=flat(soft[c]),
-                                           op0=ALU.max, op1=ALU.add)
+                                           op0=ALU.max, op1=ALU.subtract)
 
         def soft_log(c):
             nc.scalar.activation(out=flat(soft[c]), in_=flat(soft[c]), func=ACT.Ln, bias=1e-3)
@@ -142,7 +144,7 @@ def tile_deepgmm_pa_v_kernel(tc, Y, We_mu, be_mu, We_sig, be_sig, phi_mus, phi_s
         for j in range(2):
             nc.vector.scalar_tensor_tensor(out=soft[0][:, :, cols(j)], in0=a_raw[0][:, :, cols(j)], scalar=-1.0,
                                            in1=a_raw[0][:, :, cols(j)], op0=ALU.mult, op1=ALU.min)
-            nc.scalar.activation(out=soft[0][:, :, cols(j)], in_=soft[0][:, :, cols(j)], func=ACT.Exp)
+            nc.scalar.activation(out=soft[0][:, :, cols(j)], in_=soft[0][:, :, cols(j)], func=ACT.Sigmoid)
         phi_ps = bank("spare", BF16)
         for J in range(XD // P):
             nc.tensor.transpose(phi_ps[:, cols(J)], phi[:, cols(J)], ident_bf[:])
@@ -161,24 +163,28 @@ def tile_deepgmm_pa_v_kernel(tc, Y, We_mu, be_mu, We_sig, be_sig, phi_mus, phi_s
         g2_sum = keep.tile([P, 2 * PACK], F32, name="g2_sum")
         dl = keep.tile([P, 2 * PACK, KC], F32, name="dl")
         g2_rows = g2[:].rearrange("p g (t k) -> p (g t) k", k=KC)
-        nc.scalar.activation(out=flat(prob), in_=flat(zlp), func=ACT.Exp)
+        rest = keep.tile([P, 2 * PACK, KC], F32, name="rest")
+        nc.scalar.activation(out=flat(rest), in_=flat(zlp), func=ACT.Sigmoid, scale=-1.0)
+        nc.scalar.activation(out=flat(prob), in_=flat(zlp), func=ACT.Sigmoid)
+        nc.vector.reciprocal(out=rest[:], in_=rest[:])
         nc.vector.tensor_reduce(out=g2_sum[:], in_=g2_rows, axis=mybir.AxisListType.X, op=ALU.add)
         nc.vector.scalar_tensor_tensor(out=flat(minus_inv_p2), in0=flat(inv_p), scalar=-1.0, in1=flat(inv_p),
                                        op0=ALU.mult, op1=ALU.mult)
-        nc.vector.tensor_tensor(out=prob[:], in0=prob[:], in1=g2_sum[:].unsqueeze(2).to_broadcast([P, 2 * PACK, KC]),
-                                op=ALU.mult)
-        nc.vector.tensor_tensor(out=dl[:], in0=g2_rows, in1=prob[:], op=ALU.subtract)
-
+        nc.vector.tensor_tensor(out=prob[:], in0=prob[:], in1=rest[:], op=ALU.mult)
         for j in range(2):
-            nc.scalar.activation(out=soft[0][:, :, cols(j)], in_=soft[0][:, :, cols(j)], func=ACT.Ln, bias=1.0)
+            nc.scalar.activation(out=soft[0][:, :, cols(j)], in_=soft[0][:, :, cols(j)], func=ACT.Ln, scale=-1.0, bias=1.0)
             nc.vector.scalar_tensor_tensor(out=soft[0][:, :, cols(j)], in0=a_raw[0][:, :, cols(j)], scalar=0.0,
-                                           in1=soft[0][:, :, cols(j)], op0=ALU.max, op1=ALU.add)
+                                           in1=soft[0][:, :, cols(j)], op0=ALU.max, op1=ALU.subtract)
+            if j == 0:
+                nc.vector.tensor_tensor(out=prob[:], in0=prob[:], op=ALU.mult,
+                                        in1=g2_sum[:].unsqueeze(2).to_broadcast([P, 2 * PACK, KC]))
+        nc.vector.tensor_tensor(out=dl[:], in0=g2_rows, in1=prob[:], op=ALU.subtract)
         nc.scalar.activation(out=flat(ln_p), in_=flat(p_c), func=ACT.Ln)
 
         mu_ps, dl_ps, sum_mu, sum_sig = {}, {}, {}, {}
 
         def mu_features_first(c):
-            for j in range(2):
+            for j in (1, 0):
                 mu_ps[c, j] = features_first(mu_raw[c], j, "mu%d" % j)
 
         def spread_dl(i):
@@ -195,11 +201,11 @@ def tile_deepgmm_pa_v_kernel(tc, Y, We_mu, be_mu, We_sig, be_sig, phi_mus, phi_s
                                  rhs=grad[c][:, :, cols(j)], start=True, stop=False)
 
         mu_features_first(0)
-        spread_dl(0)
         new_ln_s(0)
         for j in range(2):
             head_ps = features_first(soft[0], j, "sum_mu%d" % j)
             nc.scalar.activation(out=ln_s[0][:, j, :], in_=head_ps[:], func=ACT.Ln, bias=1e-3)
+        spread_dl(0)
         open_sums(sum_sig, "sum_sig", 0, minus_ident_bf, g1_raw)
         open_sums(sum_mu, "sum_mu", 0, ident_bf, g0_raw)
 
@@ -225,10 +231,10 @@ def tile_deepgmm_pa_v_kernel(tc, Y, We_mu, be_mu, We_sig, be_sig, phi_mus, phi_s
             quantize(y_mx[g], y_grouped[g][:], E4M3)
 
         group_y(0, 0, 1, nc.vector.tensor_copy)
-        nc.vector.reciprocal(out=sig_hi[:], in_=sig_hi[:])
         quantize_y(0)
         warm_mx = mx_pair("warm", P, 1)
         quantize(warm_mx, y_grouped[0][:, 0:GROUP], E5M2)
+        nc.vector.reciprocal(out=sig_hi[:], in_=sig_hi[:])
         polish_steps = [
             lambda: nc.vector.tensor_tensor(out=guess[:], in0=sig_lo[:], in1=sig_hi[:], op=ALU.mult),
             lambda: nc.vector.scalar_tensor_tensor(out=flat(polish), in0=flat(guess), scalar=-0.5, in1=flat(guess),
@@ -238,7 +244,7 @@ def tile_deepgmm_pa_v_kernel(tc, Y, We_mu, be_mu, We_sig, be_sig, phi_mus, phi_s
                                                    op0=ALU.add, op1=ALU.mult),
         ]
 
-        share, weight, resid, square = {}, {}, {}, {}
+        share, weight, resid, square, product = {}, {}, {}, {}, {}
 
         def pair_tile(name, bufs):
             return work.tile([P, 2, GROUP], F32, name=name, tag=name, bufs=bufs)
@@ -248,44 +254,45 @@ def tile_deepgmm_pa_v_kernel(tc, Y, We_mu, be_mu, We_sig, be_sig, phi_mus, phi_s
             return table[:, 2 * (c % 2) + j, k:k + 1]
 
         def stage_share(i):
-            share[i] = pair_tile("share", 4)
+            share[i] = pair_tile("share", LEAD - AHEAD)
             for j in range(2):
                 nc.scalar.activation(out=share[i][:, j, :], in_=ln_s[i // KC][:, j, :], func=ACT.Sigmoid,
                                      scale=-1.0, bias=per_feature(ln_p, i, j))
 
         def stage_front(i):
-            weight[i] = pair_tile("weight", 5)
-            resid[i] = pair_tile("resid", 4)
-            for j in range(2):
+            factors = work.tile([P, 4, GROUP], F32, name="factors", tag="factors", bufs=AHEAD + 3)
+            weight[i], resid[i], product[i] = factors[:, 0:2, :], factors[:, 2:4, :], factors[:, 0:4:3, :]
+            for j in (1, 0):
                 nc.vector.scalar_tensor_tensor(out=weight[i][:, j, :], in0=share[i][:, j, :],
                                                scalar=per_feature(minus_inv_p2, i, j), in1=dl_ps[i][:],
                                                op0=ALU.mult, op1=ALU.mult)
                 if i == 0:
-                    polish_steps[j]()
-            for j in range(2):
+                    polish_steps[1 - j]()
+            for j in (1, 0):
                 nc.vector.scalar_tensor_tensor(out=resid[i][:, j, :], in0=mu_ps[i // KC, j][:],
                                                scalar=per_feature(phi_t[:, :, KC:2 * KC], i, j), in1=share[i][:, j, :],
                                                op0=ALU.subtract, op1=ALU.mult)
                 if i == 0:
-                    polish_steps[2 + j]()
+                    polish_steps[3 - j]()
 
         def stage_square(i):
-            square[i] = pair_tile("square", 4)
-            for j in range(2):
+            square[i] = pair_tile("square", AHEAD + 2)
+            for j in (1, 0):
                 nc.scalar.activation(out=square[i][:, j, :], in_=resid[i][:, j, :], func=ACT.Square,
                                      scale=per_feature(rsqrt_p, i, j))
 
-        def stage_back(i):
-            for j in range(2):
-                nc.vector.scalar_tensor_tensor(out=square[i][:, j, :], in0=square[i][:, j, :],
-                                               scalar=per_feature(p_c, i, j), in1=weight[i][:, j, :],
-                                               op0=ALU.subtract, op1=ALU.mult)
-            engine = nc.gpsimd if i < STEPS - 1 else nc.vector
-            engine.tensor_tensor(out=flat(weight[i]), in0=flat(weight[i]), in1=flat(resid[i]), op=ALU.mult)
+        def stage_back(i, j):
+            nc.vector.scalar_tensor_tensor(out=square[i][:, j, :], in0=square[i][:, j, :],
+                                           scalar=per_feature(p_c, i, j), in1=weight[i][:, j, :],
+                                           op0=ALU.subtract, op1=ALU.mult)
 
-        def stage_add(sums, terms, i):
+        def stage_product(engine, i, tiles, tokens):
+            engine.tensor_tensor(out=product[i][:, tiles, tokens], in0=weight[i][:, tiles, tokens],
+                                 in1=resid[i][:, tiles, tokens], op=ALU.mult)
+
+        def stage_add(sums, terms, i, tiles=(0, 1)):
             c, k = divmod(i, KC)
-            for j in range(2):
+            for j in tiles:
                 for t in range(PACK):
                     nc.tensor.matmul(sums[c, j][:, cols(t)], lhsT=terms[i][:, j, cols(t)], rhs=ident[:],
                                      is_transpose=True, start=False, stop=(k == KC - 1 and t == PACK - 1))
@@ -296,7 +303,12 @@ def tile_deepgmm_pa_v_kernel(tc, Y, We_mu, be_mu, We_sig, be_sig, phi_mus, phi_s
             if j == 0:
                 new_ln_s(c)
             turned = features_first(soft[c], j, "spare")
-            return lambda: nc.scalar.copy(out=ln_s[c][:, j, :], in_=turned[:])
+
+            def finish():
+                nc.scalar.copy(out=ln_s[c][:, j, :], in_=turned[:])
+                if j == 1:
+                    prepared.append(c)
+            return finish
 
         def gate_half(c, j):
             if j == 0:
@@ -304,15 +316,17 @@ def tile_deepgmm_pa_v_kernel(tc, Y, We_mu, be_mu, We_sig, be_sig, phi_mus, phi_s
             nc.scalar.activation(out=gate[c][:, cols(j), :], in_=a_raw[c][:, :, cols(j)].rearrange("p t d -> p d t"),
                                  func=ACT.Sigmoid)
 
-        def round_dz_sig(c):
+        def new_dz_tok(c):
             dz_tok[c] = mid([P, 2 * HALF, PACK], BF16, "dz_tok")
+
+        def round_dz_sig(c):
             for j in range(2):
                 nc.vector.scalar_tensor_tensor(out=dz_tok[c][:, cols(2 + j), :],
                                                in0=sum_sig[c, j][:].rearrange("p (t d) -> p d t", t=PACK),
                                                scalar=-1.0, in1=gate[c][:, cols(j), :], op0=ALU.mult, op1=ALU.mult)
 
-        def round_dz_mu(c):
-            for j in range(2):
+        def round_dz_mu(c, tiles=(0, 1)):
+            for j in tiles:
                 nc.scalar.copy(out=dz_tok[c][:, cols(j), :],
                                in_=sum_mu[c, j][:].rearrange("p (t d) -> p d t", t=PACK))
 
@@ -351,18 +365,19 @@ def tile_deepgmm_pa_v_kernel(tc, Y, We_mu, be_mu, We_sig, be_sig, phi_mus, phi_s
             w_mx[fh] = mx_pair("w", YD, 2)
             quantize(w_mx[fh], w_grouped[fh][:], E4M3)
 
-        def mx_group(tag, passes):
-            acc = bank(tag)
-            for n, (lhs, lhs_cols, lhs_fmt, rhs, rhs_cols, rhs_fmt) in enumerate(passes):
-                nc.tensor.matmul_mx(out=acc[:], lhsT=lhs[0][:, lhs_cols].bitcast(lhs_fmt), lhsT_scale=lhs[1][:, lhs_cols],
-                                    rhs=rhs[0][:, rhs_cols].bitcast(rhs_fmt), rhs_scale=rhs[1][:, rhs_cols],
-                                    start=(n == 0), stop=(n == len(passes) - 1))
-            return acc
+        def mx_pass(acc, lhs, lhs_cols, lhs_fmt, rhs, rhs_cols, rhs_fmt, start, stop):
+            nc.tensor.matmul_mx(out=acc[:], lhsT=lhs[0][:, lhs_cols].bitcast(lhs_fmt), lhsT_scale=lhs[1][:, lhs_cols],
+                                rhs=rhs[0][:, rhs_cols].bitcast(rhs_fmt), rhs_scale=rhs[1][:, rhs_cols],
+                                start=start, stop=stop)
+
+        def dw_pass(acc, fh, n, g):
+            mx_pass(acc, y_mx[g], cols(n), E4M3, dz_tok_mx[2 * g + fh], cols(0, GROUP), E5M2, g == 0, g == 1)
 
         def dy_group(g, n, tag, copy):
             t, h = divmod(n, 2)
-            acc = mx_group(tag, [(dz_feat_mx[2 * g + fh], cols(t), E5M2, w_mx[fh], cols(h, GROUP), E4M3)
-                                 for fh in range(2)])
+            acc = bank(tag)
+            for fh in range(2):
+                mx_pass(acc, dz_feat_mx[2 * g + fh], cols(t), E5M2, w_mx[fh], cols(h, GROUP), E4M3, fh == 0, fh == 1)
 
             def finish():
                 if h == 0:
@@ -373,23 +388,31 @@ def tile_deepgmm_pa_v_kernel(tc, Y, We_mu, be_mu, We_sig, be_sig, phi_mus, phi_s
                                       in_=flat(staged["dy", g, t]))
             return finish
 
+        def dw_open(fh, n, tag):
+            acc = bank(tag)
+            dw_pass(acc, fh, n, 0)
+            return acc
+
         def dw_group(fh, n, tag, copy):
+            return dw_close(dw_open(fh, n, tag), fh, n, copy)
+
+        def dw_close(acc, fh, n, copy):
             pair, h = divmod(n, 2)
-            acc = mx_group(tag, [(y_mx[g], cols(n), E4M3, dz_tok_mx[2 * g + fh], cols(0, GROUP), E5M2)
-                                 for g in range(2)])
+            dw_pass(acc, fh, n, 1)
 
             def finish():
-                if h == 0:
+                first = ("dw", fh, pair) not in staged
+                if first:
                     staged["dw", fh, pair] = big([P, 2, GROUP], F32, "dw_staged")
                 copy(out=staged["dw", fh, pair][:, h, :], in_=acc[:])
-                if h == 1:
+                if not first:
                     for part, dst in enumerate((out_1, out_2)):
                         rows = dst.rearrange("(y p) d -> p y d", p=P)
                         nc.sync.dma_start(out=rows[:, 2 * pair:2 * pair + 2, cols(fh, HALF)],
                                           in_=staged["dw", fh, pair][:, :, cols(part, HALF)])
             return finish
 
-        EXP_STEP, LOG_STEP = 2, 6
+        PREP_STEP, LOG_STEP = 2, 8
         spare_jobs = {}
         for n in range(2 * (CHUNKS - 1)):
             spare_jobs[LOG_STEP + 2 + n] = lambda n=n: ln_s_half(1 + n // 2, n % 2)
@@ -397,38 +420,29 @@ def tile_deepgmm_pa_v_kernel(tc, Y, We_mu, be_mu, We_sig, be_sig, phi_mus, phi_s
             for u in range(2):
                 spare_jobs[KC * (c + 1) + 2 + u] = lambda c=c, u=u: dz_feat_half(c, u, "spare", nc.scalar.copy)
         for n in range(8):
-            spare_jobs[KC + 4 + n] = lambda n=n: w_quarter(n // 4, n % 4)
-            spare_jobs[2 * KC + 5 + n] = lambda n=n: dy_group(0, n, "spare", nc.scalar.copy)
+            spare_jobs[KC + 4 + n + n // 4] = lambda n=n: w_quarter(n // 4, n % 4)
+            spare_jobs[2 * KC + 6 + n] = lambda n=n: dy_group(0, n, "spare", nc.scalar.copy)
             spare_jobs[3 * KC + 4 + n] = lambda n=n: dw_group(0, n, "spare", nc.scalar.copy)
 
         def live(i):
             return 0 <= i < STEPS
 
         def keep_warm(tag):
-            mx_group(tag, [(warm_mx, cols(0), E5M2, y_mx[0], cols(0, GROUP), E4M3)])
+            mx_pass(bank(tag), warm_mx, cols(0), E5M2, y_mx[0], cols(0, GROUP), E4M3, True, True)
 
         Y_STEP = 2 * KC + 6
-        mx_job_steps = set(range(2 * KC + 5, 2 * KC + 13)) | set(range(3 * KC + 4, 3 * KC + 12))
+        mx_job_steps = set(range(2 * KC + 6, 2 * KC + 14)) | set(range(3 * KC + 4, 3 * KC + 12))
         waiting_copy = []
-        put_off = []
-        for s in range(-2 * AHEAD, STEPS + 1):
-            scalar_away = s == LOG_STEP + 1
-            if not scalar_away:
-                for job in put_off:
-                    job()
-                put_off.clear()
-            if live(s + 2 * AHEAD):
-                if scalar_away:
-                    put_off.append(lambda i=s + 2 * AHEAD: stage_share(i))
-                else:
-                    stage_share(s + 2 * AHEAD)
+        SHARED = STEPS - 1 - AHEAD
+        both = slice(0, 2)
+        for s in range(-AHEAD - 1, STEPS - 1):
             for job in waiting_copy:
                 job()
             waiting_copy.clear()
-            if 0 <= s < CHUNKS - 1:
-                soft_abs(s + 1)
-            if live(s) and s % KC >= KC - 2:
-                gate_half(s // KC, s % 2)
+            if 0 <= s - PREP_STEP < 2 * (CHUNKS - 1):
+                (soft_abs, soft_sigmoid)[(s - PREP_STEP) % 2]((s - PREP_STEP) // 2 + 1)
+            if live(s) and s % KC in (KC - 3, KC - 2):
+                gate_half(s // KC, s % KC - (KC - 3))
             if Y_STEP <= s < Y_STEP + 8:
                 group_y(1, s - Y_STEP, 8, nc.scalar.copy)
             if s > 1 and s % KC == 1:
@@ -436,43 +450,53 @@ def tile_deepgmm_pa_v_kernel(tc, Y, We_mu, be_mu, We_sig, be_sig, phi_mus, phi_s
             if live(s + AHEAD):
                 stage_front(s + AHEAD)
             if s > 0 and s % KC == 0:
+                new_dz_tok(s // KC - 1)
                 round_dz_sig(s // KC - 1)
             if live(s + AHEAD + 1) and s + AHEAD + 1 > 0:
                 keep_warm("dl")
                 spread_dl(s + AHEAD + 1)
             if live(s + AHEAD):
-                if scalar_away:
-                    put_off.append(lambda i=s + AHEAD: stage_square(i))
-                else:
-                    stage_square(s + AHEAD)
+                stage_square(s + AHEAD)
+            if s == LOG_STEP:
+                soft_log1p(1)
+                soft_log1p(2)
+            elif s == LOG_STEP + 1:
+                soft_add_relu(1)
+                soft_log1p(3)
+                soft_log(1)
+            elif s == LOG_STEP + 2:
+                soft_add_relu(2)
+                soft_add_relu(3)
+                soft_log(2)
+                soft_log(3)
+            if not LOG_STEP <= s < LOG_STEP + 2:
+                for i in range(len(share), min(len(share) + 2, s + LEAD + 1, KC * len(prepared))):
+                    stage_share(i)
             if live(s + AHEAD + 1) and (s + AHEAD + 1) % KC == 0 and s > 0:
                 mu_features_first((s + AHEAD + 1) // KC)
-            if live(s - 1):
-                if (s - 1) % KC == 0 and s > 1:
-                    open_sums(sum_mu, "sum_mu", (s - 1) // KC, ident_bf, g0_raw)
-                stage_add(sum_mu, weight, s - 1)
-            if live(s) and s not in mx_job_steps:
-                keep_warm("spare")
-            if s == EXP_STEP:
-                for c in range(1, CHUNKS):
-                    soft_exp(c)
-            if s == LOG_STEP:
-                for c in range(1, CHUNKS):
-                    soft_log1p(c)
-            if s == LOG_STEP + 1:
-                for c in range(1, CHUNKS):
-                    soft_add_relu(c)
-                    soft_log(c)
             if live(s) and s >= KC and s % KC == 2:
                 quantize_dz_tok(s // KC - 1)
-            if live(s) and s >= KC and s % KC == 4:
+            if live(s) and s >= KC and s % KC == 5:
                 quantize_dz_feat(s // KC - 1)
-            if s in (KC + 8, KC + 12):
-                quantize_w((s - KC - 8) // 4)
-            if s == Y_STEP + 8:
+            if s in (KC + 9, KC + 14):
+                quantize_w((s - KC - 9) // 5)
+            if s == Y_STEP + 9:
                 quantize_y(1)
+            if live(s - 1):
+                if s - 1 < SHARED:
+                    stage_product(nc.vector, s - 1, both, slice(SPLIT, GROUP))
+                if (s - 1) % KC == 0 and s > 1:
+                    open_sums(sum_mu, "sum_mu", (s - 1) // KC, ident_bf, g0_raw)
+                stage_add(sum_mu, product, s - 1)
+            if live(s) and s not in mx_job_steps:
+                keep_warm("spare")
             if live(s):
-                stage_back(s)
+                for j in range(2):
+                    stage_back(s, j)
+                if s < SHARED:
+                    stage_product(nc.gpsimd, s, both, slice(0, SPLIT))
+                else:
+                    stage_product(nc.vector, s, both, slice(0, GROUP))
                 if s % KC == 0 and s > 0:
                     open_sums(sum_sig, "sum_sig", s // KC, minus_ident_bf, g1_raw)
                 stage_add(sum_sig, square, s)
@@ -482,14 +506,32 @@ def tile_deepgmm_pa_v_kernel(tc, Y, We_mu, be_mu, We_sig, be_sig, phi_mus, phi_s
                 load_chunk(s // KC + 1)
 
         last = CHUNKS - 1
-        round_dz_mu(last)
-        copy_lo = dz_feat_half(last, 0, "spare", nc.scalar.copy)
-        copy_hi = dz_feat_half(last, 1, "dl", nc.vector.tensor_copy)
+        final = STEPS - 1
+        new_dz_tok(last)
+        stage_add(sum_mu, product, final - 1)
+        opened = [dw_open(1, n, BANKS[n]) for n in range(2)]
+        for j in range(2):
+            stage_back(final, j)
+            stage_product(nc.vector, final, j, slice(0, GROUP))
+            stage_add(sum_sig, square, final, (j,))
+            stage_add(sum_mu, product, final, (j,))
+            round_dz_mu(last, (j,))
+        round_dz_sig(last)
         quantize_dz_tok(last)
+        copies = (nc.scalar.copy, nc.vector.tensor_copy)
+        copy_lo = dz_feat_half(last, 0, "spare", nc.vector.tensor_copy)
+        ready = [dw_close(opened[n], 1, n, copies[n]) for n in range(2)]
+        ready += [dw_group(1, n, BANKS[n], copies[n % 2]) for n in range(2, 4)]
+        copy_hi = dz_feat_half(last, 1, "dl", nc.scalar.copy)
+        ready[0]()
+        ready[1]()
         copy_lo()
+        ready[2]()
+        ready[3]()
         copy_hi()
+        dw_group(1, 4, BANKS[4], nc.vector.tensor_copy)()
+        dw_group(1, 5, BANKS[5], nc.vector.tensor_copy)()
         quantize_dz_feat(last)
-        for n in range(16):
-            copy = nc.scalar.copy if n % 2 == 0 else nc.vector.tensor_copy
+        for n in range(6, 16):
             group = dw_group if n < 8 else dy_group
-            group(1, n % 8, BANKS[n % 8], copy)()
+            group(1, n % 8, BANKS[n % 8], copies[n % 2])()

@@ -23,7 +23,6 @@ CHUNKS = 4
 STEPS = CHUNKS * KC
 AHEAD = 1
 LEAD = 5
-SPLIT = 448
 P_FLOOR = 2.0 ** -60
 BANKS = ("mu0", "mu1", "sum_mu0", "sum_mu1", "sum_sig0", "sum_sig1", "spare", "dl")
 
@@ -286,9 +285,9 @@ def tile_deepgmm_pa_v_kernel(tc, Y, We_mu, be_mu, We_sig, be_sig, phi_mus, phi_s
                                            scalar=per_feature(p_c, i, j), in1=weight[i][:, j, :],
                                            op0=ALU.subtract, op1=ALU.mult)
 
-        def stage_product(engine, i, tiles, tokens):
-            engine.tensor_tensor(out=product[i][:, tiles, tokens], in0=weight[i][:, tiles, tokens],
-                                 in1=resid[i][:, tiles, tokens], op=ALU.mult)
+        def stage_product(engine, i, tiles):
+            engine.tensor_tensor(out=product[i][:, tiles, :], in0=weight[i][:, tiles, :], in1=resid[i][:, tiles, :],
+                                 op=ALU.mult)
 
         def stage_add(sums, terms, i, tiles=(0, 1)):
             c, k = divmod(i, KC)
@@ -483,8 +482,6 @@ def tile_deepgmm_pa_v_kernel(tc, Y, We_mu, be_mu, We_sig, be_sig, phi_mus, phi_s
             if s == Y_STEP + 9:
                 quantize_y(1)
             if live(s - 1):
-                if s - 1 < SHARED:
-                    stage_product(nc.vector, s - 1, both, slice(SPLIT, GROUP))
                 if (s - 1) % KC == 0 and s > 1:
                     open_sums(sum_mu, "sum_mu", (s - 1) // KC, ident_bf, g0_raw)
                 stage_add(sum_mu, product, s - 1)
@@ -493,10 +490,7 @@ def tile_deepgmm_pa_v_kernel(tc, Y, We_mu, be_mu, We_sig, be_sig, phi_mus, phi_s
             if live(s):
                 for j in range(2):
                     stage_back(s, j)
-                if s < SHARED:
-                    stage_product(nc.gpsimd, s, both, slice(0, SPLIT))
-                else:
-                    stage_product(nc.vector, s, both, slice(0, GROUP))
+                stage_product(nc.gpsimd if s < SHARED else nc.vector, s, both)
                 if s % KC == 0 and s > 0:
                     open_sums(sum_sig, "sum_sig", s // KC, minus_ident_bf, g1_raw)
                 stage_add(sum_sig, square, s)
@@ -512,7 +506,7 @@ def tile_deepgmm_pa_v_kernel(tc, Y, We_mu, be_mu, We_sig, be_sig, phi_mus, phi_s
         opened = [dw_open(1, n, BANKS[n]) for n in range(2)]
         for j in range(2):
             stage_back(final, j)
-            stage_product(nc.vector, final, j, slice(0, GROUP))
+            stage_product(nc.vector, final, j)
             stage_add(sum_sig, square, final, (j,))
             stage_add(sum_mu, product, final, (j,))
             round_dz_mu(last, (j,))

@@ -231,8 +231,6 @@ def tile_deepgmm_pa_v_kernel(tc, Y, We_mu, be_mu, We_sig, be_sig, phi_mus, phi_s
 
         group_y(0, 0, 1, nc.vector.tensor_copy)
         quantize_y(0)
-        warm_mx = mx_pair("warm", P, 1)
-        quantize(warm_mx, y_grouped[0][:, 0:GROUP], E5M2)
         nc.vector.reciprocal(out=sig_hi[:], in_=sig_hi[:])
         polish_steps = [
             lambda: nc.vector.tensor_tensor(out=guess[:], in0=sig_lo[:], in1=sig_hi[:], op=ALU.mult),
@@ -426,11 +424,7 @@ def tile_deepgmm_pa_v_kernel(tc, Y, We_mu, be_mu, We_sig, be_sig, phi_mus, phi_s
         def live(i):
             return 0 <= i < STEPS
 
-        def keep_warm(tag):
-            mx_pass(bank(tag), warm_mx, cols(0), E5M2, y_mx[0], cols(0, GROUP), E4M3, True, True)
-
         Y_STEP = 2 * KC + 6
-        mx_job_steps = set(range(2 * KC + 6, 2 * KC + 14)) | set(range(3 * KC + 4, 3 * KC + 12))
         waiting_copy = []
         SHARED = STEPS - 1 - AHEAD
         both = slice(0, 2)
@@ -452,7 +446,6 @@ def tile_deepgmm_pa_v_kernel(tc, Y, We_mu, be_mu, We_sig, be_sig, phi_mus, phi_s
                 new_dz_tok(s // KC - 1)
                 round_dz_sig(s // KC - 1)
             if live(s + AHEAD + 1) and s + AHEAD + 1 > 0:
-                keep_warm("dl")
                 spread_dl(s + AHEAD + 1)
             if live(s + AHEAD):
                 stage_square(s + AHEAD)
@@ -485,8 +478,6 @@ def tile_deepgmm_pa_v_kernel(tc, Y, We_mu, be_mu, We_sig, be_sig, phi_mus, phi_s
                 if (s - 1) % KC == 0 and s > 1:
                     open_sums(sum_mu, "sum_mu", (s - 1) // KC, ident_bf, g0_raw)
                 stage_add(sum_mu, product, s - 1)
-            if live(s) and s not in mx_job_steps:
-                keep_warm("spare")
             if live(s):
                 for j in range(2):
                     stage_back(s, j)

from contextlib import ExitStack

import concourse.mybir as mybir
from concourse.masks import make_identity

N, KC, YD, XD = 1024, 16, 1024, 512
FLOPS = 2 * 2 * N * YD * 2 * XD

F32 = mybir.dt.float32
BF16 = mybir.dt.bfloat16
U32 = mybir.dt.uint32
U8 = mybir.dt.uint8
E4M3 = mybir.dt.float8_e4m3fn_x4
E5M2 = mybir.dt.float8_e5m2_x4
ALU = mybir.AluOpType
ACT = mybir.ActivationFunctionType

P = 128
PACK = 4
GROUP = P * PACK
HALF = XD // 2
CHUNKS = 4
STEPS = CHUNKS * KC
AHEAD = 1
LEAD = 5
P_FLOOR = 2.0 ** -60
BANKS = ("mu0", "mu1", "sum_mu0", "sum_mu1", "sum_sig0", "sum_sig1", "spare", "dl")


def tile_deepgmm_pa_v_kernel(tc, Y, We_mu, be_mu, We_sig, be_sig, phi_mus, phi_sigs, phi_logits,
                                          enc_mu, sig_pre, z_log_probs, grad_0, grad_1, grad_2,
                                          out_0, out_1, out_2):
    nc = tc.nc

    def chunk_rows(dram, c):
        g, fh = divmod(c, 2)
        return dram.rearrange("(g p t) w -> g p t w", g=2, t=PACK)[g, :, :, fh * HALF:(fh + 1) * HALF]

    def cols(n, width=P):
        return slice(n * width, (n + 1) * width)

    with ExitStack() as ctx:
        keep = ctx.enter_context(tc.tile_pool(name="keep", bufs=1))
        work = ctx.enter_context(tc.tile_pool(name="work", bufs=1))
        psum = ctx.enter_context(tc.psum_pool(name="psum", bufs=1))
        ctx.enter_context(tc.manual_schedule())

        def bank(tag, dtype=F32):
            return psum.tile([P, GROUP], dtype, name=tag, tag=tag)

        def big(shape, dtype, name):
            return work.tile(shape, dtype, name=name, tag="big", bufs=5, align_bytes=64)

        def mid(shape, dtype, name):
            return work.tile(shape, dtype, name=name, tag="mid", bufs=3, align_bytes=64)

        def to_quantize(name):
            return work.tile([P, PACK * YD], BF16, name=name, tag="to_quantize", bufs=1, align_bytes=64)

        def mx_pair(name, width, bufs):
            codes = work.tile([P, width], U32, name=name + "_codes", tag=name + "_codes", bufs=bufs, align_bytes=64)
            scales = work.tile([P, width], U8, name=name + "_scales", tag=name + "_scales", bufs=bufs, align_bytes=64)
            return codes, scales

        a_raw = [keep.tile([P, PACK, HALF], F32, name="a_raw%d" % c) for c in range(CHUNKS)]
        phi = keep.tile([P, XD], BF16, name="phi")
        zlp = keep.tile([P, 2, PACK * KC], F32, name="zlp")
        g2 = keep.tile([P, 2, PACK * KC], BF16, name="g2")
        mu_raw, g0_raw, g1_raw, y_raw, w_raw = {}, {}, {}, {}, {}

        def load_chunk(c):
            mu_raw[c] = work.tile([P, PACK, HALF], F32, name="mu_raw", tag="mu_raw", bufs=1)
            g0_raw[c] = work.tile([P, PACK, HALF], BF16, name="g0_raw", tag="g0_raw", bufs=1)
            g1_raw[c] = work.tile([P, PACK, HALF], BF16, name="g1_raw", tag="g1_raw", bufs=1)
            nc.sync.dma_start(out=mu_raw[c][:], in_=chunk_rows(enc_mu, c))
            nc.sync.dma_start(out=g1_raw[c][:], in_=chunk_rows(grad_1, c))
            nc.sync.dma_start(out=g0_raw[c][:], in_=chunk_rows(grad_0, c))

        def load_y(g):
            y_raw[g] = big([P, PACK, YD], BF16, "y_raw")
            nc.sync.dma_start(out=y_raw[g][:], in_=Y.rearrange("(g p t) w -> g p t w", g=2, t=PACK)[g])

        def load_w(fh):
            w_raw[fh] = big([P, YD // P, 2 * HALF], BF16, "w_raw")
            for part, weight in enumerate((We_mu, We_sig)):
                nc.sync.dma_start(out=w_raw[fh][:, :, cols(part, HALF)],
                                  in_=weight.rearrange("(y p) c -> p y c", p=P)[:, :, cols(fh, HALF)])

        nc.vector.memset(phi[:], 0.0)
        for j in range(2):
            nc.sync.dma_start(out=a_raw[0][:, :, cols(j)], in_=chunk_rows(sig_pre, 0)[:, :, cols(j)])
        nc.sync.dma_start(out=phi[0:KC, :], in_=phi_sigs)
        nc.sync.dma_start(out=phi[KC:2 * KC, :], in_=phi_mus)
        nc.sync.dma_start(out=zlp[:], in_=z_log_probs.rearrange("(g p t) k -> p g (t k)", g=2, t=PACK))
        nc.sync.dma_start(out=g2[:], in_=grad_2.rearrange("(g p t) k -> p g (t k)", g=2, t=PACK))
        load_chunk(0)
        load_y(0)
        for c in range(1, CHUNKS):
            nc.sync.dma_start(out=a_raw[c][:], in_=chunk_rows(sig_pre, c))
        load_w(0)
        load_w(1)
        load_y(1)

        ident = keep.tile([P, P], F32, name="ident")
        ident_bf = keep.tile([P, P], BF16, name="ident_bf")
        minus_ident_bf = keep.tile([P, P], BF16, name="minus_ident_bf")
        make_identity(nc, ident_bf[:])
        make_identity(nc, ident[:])
        nc.vector.tensor_scalar(out=minus_ident_bf[:], in0=ident_bf[:], scalar1=-1.0, scalar2=None, op0=ALU.mult)

        soft, ln_s, prepared = {}, {}, [0]

        def flat(tile3):
            return tile3[:].rearrange("p a b -> p (a b)")

        def soft_abs(c):
            soft[c] = mid([P, PACK, HALF], F32, "soft")
            nc.scalar.activation(out=flat(soft[c]), in_=flat(a_raw[c]), func=ACT.Abs)

        def soft_sigmoid(c):
            nc.scalar.activation(out=flat(soft[c]), in_=flat(soft[c]), func=ACT.Sigmoid, scale=-1.0)

        def soft_log1p(c):
            nc.scalar.activation(out=flat(soft[c]), in_=flat(soft[c]), func=ACT.Ln, scale=-1.0, bias=1.0)

        def soft_add_relu(c):
            nc.vector.scalar_tensor_tensor(out=flat(soft[c]), in0=flat(a_raw[c]), scalar=0.0, in1=flat(soft[c]),
                                           op0=ALU.max, op1=ALU.subtract)

        def soft_log(c):
            nc.scalar.activation(out=flat(soft[c]), in_=flat(soft[c]), func=ACT.Ln, bias=1e-3)

        def features_first(src, j, tag):
            dst = bank(tag)
            for t in range(PACK):
                nc.tensor.transpose(dst[:, cols(t)], src[:, t, cols(j)], ident[:])
            return dst

        def new_ln_s(c):
            ln_s[c] = keep.tile([P, 2, GROUP], F32, name="ln_s%d" % c)

        soft[0] = mid([P, PACK, HALF], F32, "soft")
        for j in range(2):
            nc.vector.scalar_tensor_tensor(out=soft[0][:, :, cols(j)], in0=a_raw[0][:, :, cols(j)], scalar=-1.0,
                                           in1=a_raw[0][:, :, cols(j)], op0=ALU.mult, op1=ALU.min)
            nc.scalar.activation(out=soft[0][:, :, cols(j)], in_=soft[0][:, :, cols(j)], func=ACT.Sigmoid)
        phi_ps = bank("spare", BF16)
        for J in range(XD // P):
            nc.tensor.transpose(phi_ps[:, cols(J)], phi[:, cols(J)], ident_bf[:])
        phi_t = keep.tile([P, XD // P, 2 * KC], F32, name="phi_t")
        nc.vector.tensor_copy(out=phi_t[:], in_=phi_ps[:].rearrange("d (J r) -> d J r", r=P)[:, :, 0:2 * KC])

        def small(name):
            return keep.tile([P, XD // P, KC], F32, name=name)

        p_c, ln_p, inv_p, minus_inv_p2 = small("p_c"), small("ln_p"), small("inv_p"), small("minus_inv_p2")
        sig_lo, sig_hi, guess, polish, rsqrt_p = small("sig_lo"), small("sig_hi"), small("guess"), small("polish"), small("rsqrt_p")
        nc.vector.tensor_scalar(out=p_c[:], in0=phi_t[:, :, 0:KC], scalar1=P_FLOOR, scalar2=None, op0=ALU.max)
        nc.vector.reciprocal(out=inv_p[:], in_=p_c[:])

        prob = keep.tile([P, 2 * PACK, KC], F32, name="prob")
        g2_sum = keep.tile([P, 2 * PACK], F32, name="g2_sum")
        dl = keep.tile([P, 2 * PACK, KC], F32, name="dl")
        g2_rows = g2[:].rearrange("p g (t k) -> p (g t) k", k=KC)
        rest = keep.tile([P, 2 * PACK, KC], F32, name="rest")
        nc.scalar.activation(out=flat(rest), in_=flat(zlp), func=ACT.Sigmoid, scale=-1.0)
        nc.scalar.activation(out=flat(prob), in_=flat(zlp), func=ACT.Sigmoid)
        nc.vector.reciprocal(out=rest[:], in_=rest[:])
        nc.vector.tensor_reduce(out=g2_sum[:], in_=g2_rows, axis=mybir.AxisListType.X, op=ALU.add)
        nc.vector.scalar_tensor_tensor(out=flat(minus_inv_p2), in0=flat(inv_p), scalar=-1.0, in1=flat(inv_p),
                                       op0=ALU.mult, op1=ALU.mult)
        nc.vector.tensor_tensor(out=prob[:], in0=prob[:], in1=rest[:], op=ALU.mult)
        for j in range(2):
            nc.scalar.activation(out=soft[0][:, :, cols(j)], in_=soft[0][:, :, cols(j)], func=ACT.Ln, scale=-1.0, bias=1.0)
            nc.vector.scalar_tensor_tensor(out=soft[0][:, :, cols(j)], in0=a_raw[0][:, :, cols(j)], scalar=0.0,
                                           in1=soft[0][:, :, cols(j)], op0=ALU.max, op1=ALU.subtract)
            if j == 0:
                nc.vector.tensor_tensor(out=prob[:], in0=prob[:], op=ALU.mult,
                                        in1=g2_sum[:].unsqueeze(2).to_broadcast([P, 2 * PACK, KC]))
        nc.vector.tensor_tensor(out=dl[:], in0=g2_rows, in1=prob[:], op=ALU.subtract)
        nc.scalar.activation(out=flat(ln_p), in_=flat(p_c), func=ACT.Ln)

        mu_ps, dl_ps, sum_mu, sum_sig = {}, {}, {}, {}

        def mu_features_first(c):
            for j in (1, 0):
                mu_ps[c, j] = features_first(mu_raw[c], j, "mu%d" % j)

        def spread_dl(i):
            c, k = divmod(i, KC)
            dl_ps[i] = bank("dl")
            for t in range(PACK):
                column = dl[:, PACK * (c // 2) + t, k:k + 1]
                nc.tensor.transpose(dl_ps[i][:, cols(t)], column.to_broadcast([P, P]), ident[:])

        def open_sums(sums, tag, c, sign, grad):
            for j in range(2):
                sums[c, j] = bank("%s%d" % (tag, j))
                nc.tensor.matmul(sums[c, j][:].rearrange("p (t d) -> p t d", t=PACK), lhsT=sign[:],
                                 rhs=grad[c][:, :, cols(j)], start=True, stop=False)

        mu_features_first(0)
        new_ln_s(0)
        for j in range(2):
            head_ps = features_first(soft[0], j, "sum_mu%d" % j)
            nc.scalar.activation(out=ln_s[0][:, j, :], in_=head_ps[:], func=ACT.Ln, bias=1e-3)
        spread_dl(0)
        open_sums(sum_sig, "sum_sig", 0, minus_ident_bf, g1_raw)
        open_sums(sum_mu, "sum_mu", 0, ident_bf, g0_raw)

        nc.scalar.activation(out=flat(sig_lo), in_=flat(ln_p), func=ACT.Sigmoid, scale=-0.5)
        nc.scalar.activation(out=flat(sig_hi), in_=flat(ln_p), func=ACT.Sigmoid, scale=0.5)

        y_mx, w_mx, dz_tok_mx, dz_feat_mx = {}, {}, {}, {}

        def quantize(pair, src, fmt):
            nc.vector.quantize_mx(out=pair[0][:].bitcast(fmt), scales=pair[1][:], in_=src)

        y_grouped = {}

        def group_y(g, n, parts, copy):
            if n == 0:
                y_grouped[g] = to_quantize("y_grouped")
            width = YD // parts
            copy(out=y_grouped[g][:, cols(n, PACK * width)].rearrange("p (c i t) -> p c t i", i=4, t=PACK),
                 in_=y_raw[g][:, :, cols(n, width)].rearrange("p t (c i) -> p c t i", i=4))

        def quantize_y(g):
            y_mx[g] = mx_pair("y", YD, 2)
            quantize(y_mx[g], y_grouped[g][:], E4M3)

        group_y(0, 0, 1, nc.vector.tensor_copy)
        quantize_y(0)
        nc.vector.reciprocal(out=sig_hi[:], in_=sig_hi[:])
        polish_steps = [
            lambda: nc.vector.tensor_tensor(out=guess[:], in0=sig_lo[:], in1=sig_hi[:], op=ALU.mult),
            lambda: nc.vector.scalar_tensor_tensor(out=flat(polish), in0=flat(guess), scalar=-0.5, in1=flat(guess),
                                                   op0=ALU.mult, op1=ALU.mult),
            lambda: nc.vector.tensor_tensor(out=polish[:], in0=polish[:], in1=p_c[:], op=ALU.mult),
            lambda: nc.vector.scalar_tensor_tensor(out=flat(rsqrt_p), in0=flat(polish), scalar=1.5, in1=flat(guess),
                                                   op0=ALU.add, op1=ALU.mult),
        ]

        share, weight, resid, square, product = {}, {}, {}, {}, {}

        def pair_tile(name, bufs):
            return work.tile([P, 2, GROUP], F32, name=name, tag=name, bufs=bufs)

        def per_feature(table, i, j):
            c, k = divmod(i, KC)
            return table[:, 2 * (c % 2) + j, k:k + 1]

        def stage_share(i):
            share[i] = pair_tile("share", LEAD - AHEAD)
            for j in range(2):
                nc.scalar.activation(out=share[i][:, j, :], in_=ln_s[i // KC][:, j, :], func=ACT.Sigmoid,
                                     scale=-1.0, bias=per_feature(ln_p, i, j))

        def stage_front(i):
            factors = work.tile([P, 4, GROUP], F32, name="factors", tag="factors", bufs=AHEAD + 3)
            weight[i], resid[i], product[i] = factors[:, 0:2, :], factors[:, 2:4, :], factors[:, 0:4:3, :]
            for j in (1, 0):
                nc.vector.scalar_tensor_tensor(out=weight[i][:, j, :], in0=share[i][:, j, :],
                                               scalar=per_feature(minus_inv_p2, i, j), in1=dl_ps[i][:],
                                               op0=ALU.mult, op1=ALU.mult)
                if i == 0:
                    polish_steps[1 - j]()
            for j in (1, 0):
                nc.vector.scalar_tensor_tensor(out=resid[i][:, j, :], in0=mu_ps[i // KC, j][:],
                                               scalar=per_feature(phi_t[:, :, KC:2 * KC], i, j), in1=share[i][:, j, :],
                                               op0=ALU.subtract, op1=ALU.mult)
                if i == 0:
                    polish_steps[3 - j]()

        def stage_square(i):
            square[i] = pair_tile("square", AHEAD + 2)
            for j in (1, 0):
                nc.scalar.activation(out=square[i][:, j, :], in_=resid[i][:, j, :], func=ACT.Square,
                                     scale=per_feature(rsqrt_p, i, j))

        def stage_back(i, j):
            nc.vector.scalar_tensor_tensor(out=square[i][:, j, :], in0=square[i][:, j, :],
                                           scalar=per_feature(p_c, i, j), in1=weight[i][:, j, :],
                                           op0=ALU.subtract, op1=ALU.mult)

        def stage_product(engine, i, tiles):
            engine.tensor_tensor(out=product[i][:, tiles, :], in0=weight[i][:, tiles, :], in1=resid[i][:, tiles, :],
                                 op=ALU.mult)

        def stage_add(sums, terms, i, tiles=(0, 1)):
            c, k = divmod(i, KC)
            for j in tiles:
                for t in range(PACK):
                    nc.tensor.matmul(sums[c, j][:, cols(t)], lhsT=terms[i][:, j, cols(t)], rhs=ident[:],
                                     is_transpose=True, start=False, stop=(k == KC - 1 and t == PACK - 1))

        gate, dz_tok, dz_feat, w_grouped, staged = {}, {}, {}, {}, {}

        def ln_s_half(c, j):
            if j == 0:
                new_ln_s(c)
            turned = features_first(soft[c], j, "spare")

            def finish():
                nc.scalar.copy(out=ln_s[c][:, j, :], in_=turned[:])
                if j == 1:
                    prepared.append(c)
            return finish

        def gate_half(c, j):
            if j == 0:
                gate[c] = work.tile([P, HALF, PACK], F32, name="gate", tag="gate", bufs=1)
            nc.scalar.activation(out=gate[c][:, cols(j), :], in_=a_raw[c][:, :, cols(j)].rearrange("p t d -> p d t"),
                                 func=ACT.Sigmoid)

        def new_dz_tok(c):
            dz_tok[c] = mid([P, 2 * HALF, PACK], BF16, "dz_tok")

        def round_dz_sig(c):
            for j in range(2):
                nc.vector.scalar_tensor_tensor(out=dz_tok[c][:, cols(2 + j), :],
                                               in0=sum_sig[c, j][:].rearrange("p (t d) -> p d t", t=PACK),
                                               scalar=-1.0, in1=gate[c][:, cols(j), :], op0=ALU.mult, op1=ALU.mult)

        def round_dz_mu(c, tiles=(0, 1)):
            for j in tiles:
                nc.scalar.copy(out=dz_tok[c][:, cols(j), :],
                               in_=sum_mu[c, j][:].rearrange("p (t d) -> p d t", t=PACK))

        def quantize_dz_tok(c):
            dz_tok_mx[c] = mx_pair("dz_tok", GROUP, CHUNKS)
            quantize(dz_tok_mx[c], flat(dz_tok[c]), E5M2)

        def dz_feat_half(c, u, tag, copy):
            if u == 0:
                dz_feat[c] = mid([P, GROUP, PACK], BF16, "dz_feat")
            words = flat(dz_tok[c]).bitcast(F32)
            turned = bank(tag)
            for f in range(PACK):
                nc.tensor.transpose(turned[:, cols(f)], words[:, 2 * f + u:2 * GROUP:2 * PACK], ident[:])
            return lambda: copy(out=dz_feat[c][:, cols(u, 2 * P), :].rearrange("q (e p) f -> q e p f", e=2),
                                in_=turned[:].bitcast(BF16).rearrange("q (f p e) -> q e p f", f=PACK, e=2))

        def quantize_dz_feat(c):
            dz_feat_mx[c] = mx_pair("dz_feat", GROUP, 2)
            quantize(dz_feat_mx[c], flat(dz_feat[c]), E5M2)

        def w_quarter(fh, n):
            if n == 0:
                w_grouped[fh] = to_quantize("w_grouped")
            words = flat(w_raw[fh]).bitcast(F32)
            turned = bank("spare")
            for y in range(2):
                for u in range(2):
                    first = HALF * (2 * n + y)
                    nc.tensor.transpose(turned[:, cols(2 * y + u)], words[:, first + u:first + HALF:2], ident[:])
            return lambda: nc.scalar.copy(
                out=w_grouped[fh][:].bitcast(F32)[:, cols(n, GROUP)].rearrange("q (y p u) -> q y p u", y=2, u=2),
                in_=turned[:].rearrange("q (y u p) -> q y p u", y=2, u=2))

        def quantize_w(fh):
            w_mx[fh] = mx_pair("w", YD, 2)
            quantize(w_mx[fh], w_grouped[fh][:], E4M3)

        def mx_pass(acc, lhs, lhs_cols, lhs_fmt, rhs, rhs_cols, rhs_fmt, start, stop):
            nc.tensor.matmul_mx(out=acc[:], lhsT=lhs[0][:, lhs_cols].bitcast(lhs_fmt), lhsT_scale=lhs[1][:, lhs_cols],
                                rhs=rhs[0][:, rhs_cols].bitcast(rhs_fmt), rhs_scale=rhs[1][:, rhs_cols],
                                start=start, stop=stop)

        def dw_pass(acc, fh, n, g):
            mx_pass(acc, y_mx[g], cols(n), E4M3, dz_tok_mx[2 * g + fh], cols(0, GROUP), E5M2, g == 0, g == 1)

        def dy_group(g, n, tag, copy):
            t, h = divmod(n, 2)
            acc = bank(tag)
            for fh in range(2):
                mx_pass(acc, dz_feat_mx[2 * g + fh], cols(t), E5M2, w_mx[fh], cols(h, GROUP), E4M3, fh == 0, fh == 1)

            def finish():
                if h == 0:
                    staged["dy", g, t] = big([P, 2, GROUP], F32, "dy_staged")
                copy(out=staged["dy", g, t][:, h, :], in_=acc[:])
                if h == 1:
                    nc.sync.dma_start(out=out_0.rearrange("(g p t) y -> g t p y", g=2, t=PACK)[g, t],
                                      in_=flat(staged["dy", g, t]))
            return finish

        def dw_open(fh, n, tag):
            acc = bank(tag)
            dw_pass(acc, fh, n, 0)
            return acc

        def dw_group(fh, n, tag, copy):
            return dw_close(dw_open(fh, n, tag), fh, n, copy)

        def dw_close(acc, fh, n, copy):
            pair, h = divmod(n, 2)
            dw_pass(acc, fh, n, 1)

            def finish():
                first = ("dw", fh, pair) not in staged
                if first:
                    staged["dw", fh, pair] = big([P, 2, GROUP], F32, "dw_staged")
                copy(out=staged["dw", fh, pair][:, h, :], in_=acc[:])
                if not first:
                    for part, dst in enumerate((out_1, out_2)):
                        rows = dst.rearrange("(y p) d -> p y d", p=P)
                        nc.sync.dma_start(out=rows[:, 2 * pair:2 * pair + 2, cols(fh, HALF)],
                                          in_=staged["dw", fh, pair][:, :, cols(part, HALF)])
            return finish

        PREP_STEP, LOG_STEP = 2, 8
        spare_jobs = {}
        for n in range(2 * (CHUNKS - 1)):
            spare_jobs[LOG_STEP + 2 + n] = lambda n=n: ln_s_half(1 + n // 2, n % 2)
        for c in range(CHUNKS - 1):
            for u in range(2):
                spare_jobs[KC * (c + 1) + 2 + u] = lambda c=c, u=u: dz_feat_half(c, u, "spare", nc.scalar.copy)
        for n in range(8):
            spare_jobs[KC + 4 + n + n // 4] = lambda n=n: w_quarter(n // 4, n % 4)
            spare_jobs[2 * KC + 6 + n] = lambda n=n: dy_group(0, n, "spare", nc.scalar.copy)
            spare_jobs[3 * KC + 4 + n] = lambda n=n: dw_group(0, n, "spare", nc.scalar.copy)

        def live(i):
            return 0 <= i < STEPS

        Y_STEP = 2 * KC + 6
        waiting_copy = []
        SHARED = STEPS - 1 - AHEAD
        both = slice(0, 2)
        for s in range(-AHEAD - 1, STEPS - 1):
            for job in waiting_copy:
                job()
            waiting_copy.clear()
            if 0 <= s - PREP_STEP < 2 * (CHUNKS - 1):
                (soft_abs, soft_sigmoid)[(s - PREP_STEP) % 2]((s - PREP_STEP) // 2 + 1)
            if live(s) and s % KC in (KC - 3, KC - 2):
                gate_half(s // KC, s % KC - (KC - 3))
            if Y_STEP <= s < Y_STEP + 8:
                group_y(1, s - Y_STEP, 8, nc.scalar.copy)
            if s > 1 and s % KC == 1:
                round_dz_mu(s // KC - 1)
            if live(s + AHEAD):
                stage_front(s + AHEAD)
            if s > 0 and s % KC == 0:
                new_dz_tok(s // KC - 1)
                round_dz_sig(s // KC - 1)
            if live(s + AHEAD + 1) and s + AHEAD + 1 > 0:
                spread_dl(s + AHEAD + 1)
            if live(s + AHEAD):
                stage_square(s + AHEAD)
            if s == LOG_STEP:
                soft_log1p(1)
                soft_log1p(2)
            elif s == LOG_STEP + 1:
                soft_add_relu(1)
                soft_log1p(3)
                soft_log(1)
            elif s == LOG_STEP + 2:
                soft_add_relu(2)
                soft_add_relu(3)
                soft_log(2)
                soft_log(3)
            if not LOG_STEP <= s < LOG_STEP + 2:
                for i in range(len(share), min(len(share) + 2, s + LEAD + 1, KC * len(prepared))):
                    stage_share(i)
            if live(s + AHEAD + 1) and (s + AHEAD + 1) % KC == 0 and s > 0:
                mu_features_first((s + AHEAD + 1) // KC)
            if live(s) and s >= KC and s % KC == 2:
                quantize_dz_tok(s // KC - 1)
            if live(s) and s >= KC and s % KC == 5:
                quantize_dz_feat(s // KC - 1)
            if s in (KC + 9, KC + 14):
                quantize_w((s - KC - 9) // 5)
            if s == Y_STEP + 9:
                quantize_y(1)
            if live(s - 1):
                if (s - 1) % KC == 0 and s > 1:
                    open_sums(sum_mu, "sum_mu", (s - 1) // KC, ident_bf, g0_raw)
                stage_add(sum_mu, product, s - 1)
            if live(s):
                for j in range(2):
                    stage_back(s, j)
                stage_product(nc.gpsimd if s < SHARED else nc.vector, s, both)
                if s % KC == 0 and s > 0:
                    open_sums(sum_sig, "sum_sig", s // KC, minus_ident_bf, g1_raw)
                stage_add(sum_sig, square, s)
            if s in spare_jobs:
                waiting_copy.append(spare_jobs[s]())
            if live(s) and s % KC == 4 and s // KC + 1 < CHUNKS:
                load_chunk(s // KC + 1)

        last = CHUNKS - 1
        final = STEPS - 1
        new_dz_tok(last)
        stage_add(sum_mu, product, final - 1)
        opened = [dw_open(1, n, BANKS[n]) for n in range(2)]
        for j in range(2):
            stage_back(final, j)
            stage_product(nc.vector, final, j)
            stage_add(sum_sig, square, final, (j,))
            stage_add(sum_mu, product, final, (j,))
            round_dz_mu(last, (j,))
        round_dz_sig(last)
        quantize_dz_tok(last)
        copies = (nc.scalar.copy, nc.vector.tensor_copy)
        copy_lo = dz_feat_half(last, 0, "spare", nc.vector.tensor_copy)
        ready = [dw_close(opened[n], 1, n, copies[n]) for n in range(2)]
        ready += [dw_group(1, n, BANKS[n], copies[n % 2]) for n in range(2, 4)]
        copy_hi = dz_feat_half(last, 1, "dl", nc.scalar.copy)
        ready[0]()
        ready[1]()
        copy_lo()
        ready[2]()
        ready[3]()
        copy_hi()
        dw_group(1, 4, BANKS[4], nc.vector.tensor_copy)()
        dw_group(1, 5, BANKS[5], nc.vector.tensor_copy)()
        quantize_dz_feat(last)
        for n in range(6, 16):
            group = dw_group if n < 8 else dy_group
            group(1, n % 8, BANKS[n % 8], copies[n % 2])()
